import numpy as np
import ml_dtypes


def mxq(x, axis, fmt="e4m3"):
    dtype, down = {"e4m3": (ml_dtypes.float8_e4m3fn, 7), "e5m2": (ml_dtypes.float8_e5m2, 14)}[fmt]
    v = np.moveaxis(np.asarray(x, np.float32).astype(ml_dtypes.bfloat16).astype(np.float64), axis, -1)
    blocks = v.reshape(v.shape[:-1] + (-1, 32))
    amax = np.abs(blocks).max(-1, keepdims=True)
    byte = np.maximum(np.where(amax > 0, np.frexp(amax)[1] - 1 + 127, 0) - down, 1)
    scale = np.exp2(byte - 127.0)
    codes = (blocks / scale).astype(np.float32).astype(dtype).astype(np.float64)
    return np.moveaxis((codes * scale).reshape(v.shape), -1, axis)


WIDE = False


def mx_kscale(k):
    if not WIDE:
        return np.ones(k)
    levels = np.array([20, -20, 10, -10, 0])
    a = np.random.permutation(np.resize(levels, k // 512 * 4)).reshape(k // 512, 4)
    idx = np.arange(k)
    return np.exp2(a[idx // 512, idx % 128 // 32])


BF16 = ml_dtypes.bfloat16


def bf(x):
    return np.asarray(x, np.float32).astype(BF16)


def f64(x):
    return np.asarray(x).astype(np.float64)


N, K, H = 1024, 8, 512


def sigmoid(v):
    return 1.0 / (1.0 + np.exp(-v))


def cell_parts(mh, mc, w_iou, bias_iou, w_f, bias_f):
    hc = np.concatenate([mh.sum(axis=1), mh.max(axis=1)], axis=1)
    f = sigmoid(hc @ w_f.T + bias_f)
    c_agg = np.sum(f[:, None, :] * mc, axis=1)
    iou = hc @ w_iou.T + bias_iou
    i, o, u = np.split(iou, 3, axis=1)
    c = sigmoid(i) * np.tanh(u) + c_agg
    h = sigmoid(o) * np.tanh(c)
    return iou, c, h


def setup_inputs():
    s = mx_kscale(N)
    w = 1.0 / np.sqrt(H * (K + 2))
    mh0 = bf(np.random.standard_normal((N, K, H)))
    mc = bf(np.random.standard_normal((N, K, H)) / np.sqrt(K))
    w_iou = bf(np.random.standard_normal((3 * H, 2 * H)) * w)
    bias_iou = bf(np.random.standard_normal((1, 3 * H)) * 0.1)
    w_f = bf(np.random.standard_normal((H, 2 * H)) * w)
    bias_f = bf(np.random.standard_normal(H) * 0.1)
    g = bf(np.random.standard_normal((N, 2 * H)) * np.exp2(np.random.randint(-12, 1, (N, 1))) / s[:, None])
    iou, c, _ = cell_parts(f64(mh0), f64(mc), f64(w_iou), f64(bias_iou), f64(w_f), f64(bias_f))
    return {"mailbox_h": bf(f64(mh0) * s[:, None, None]),
            "mailbox_c": mc,
            "U_iou_w": w_iou,
            "b_iou": bias_iou,
            "U_f_w": w_f,
            "U_f_b": bias_f,
            "iou": np.asarray(iou, np.float32),
            "c": np.asarray(c, np.float32),
            "grad_out": g}


def reference(mailbox_h, mailbox_c, U_iou_w, b_iou, U_f_w, U_f_b, iou, c, grad_out):
    mh = f64(mailbox_h)
    hc = np.concatenate([mh.sum(axis=1), mh.max(axis=1)], axis=1)
    i, o, u = np.split(f64(iou), 3, axis=1)
    g = f64(grad_out)
    gh = g[:, :H]
    gc = g[:, H:]
    si = sigmoid(i)
    so = sigmoid(o)
    tu = np.tanh(u)
    tc = np.tanh(f64(c))
    dc = gc + gh * so * (1.0 - tc * tc)
    di = dc * tu * si * (1.0 - si)
    do = gh * tc * so * (1.0 - so)
    du = dc * si * (1.0 - tu * tu)
    diou = np.concatenate([di, do, du], axis=1)
    return mxq(diou, 0, "e5m2").T @ mxq(hc, 0, "e4m3")

@@ -1,0 +1,171 @@
+from contextlib import ExitStack
+
+import concourse.mybir as mybir
+
+F32 = mybir.dt.float32
+BF16 = mybir.dt.bfloat16
+U32 = mybir.dt.uint32
+U8 = mybir.dt.uint8
+E4M3X4 = mybir.dt.float8_e4m3fn_x4
+E5M2X4 = mybir.dt.float8_e5m2_x4
+ADD = mybir.AluOpType.add
+MULT = mybir.AluOpType.mult
+MAX = mybir.AluOpType.max
+TANH = mybir.ActivationFunctionType.Tanh
+SQUARE = mybir.ActivationFunctionType.Square
+
+P = 128
+PACK = 4
+NODES = 1024
+CHILDREN = 8
+H = 512
+PASSES = NODES // (P * PACK)
+BANK = 512
+RUN = 4
+MAIL_BUFS = 3
+
+FLOPS = 2 * 3 * H * 2 * H * NODES
+BYTES = 2 * NODES * CHILDREN * H + 4 * NODES * 3 * H + 4 * NODES * H + 2 * NODES * 2 * H + 4 * 3 * H * 2 * H
+
+
+def regroup(nc, grouped, rows):
+    nc.scalar.copy(
+        out=grouped.rearrange("p (b i) j -> p b j i", i=RUN),
+        in_=rows.rearrange("p j (b i) -> p b j i", i=RUN),
+    )
+
+
+def tile_treelstmcellv2_v_kernel(
+    tc, mailbox_h, mailbox_c, U_iou_w, b_iou, U_f_w, U_f_b, iou, c, grad_out, out
+):
+    nc = tc.nc
+    mail_v = mailbox_h.rearrange("(k p j) ch h -> k j p ch h", p=P, j=PACK)
+    iou_v = iou.rearrange("(k p j) w -> k p j w", p=P, j=PACK)
+    cell_v = c.rearrange("(k p j) w -> k p j w", p=P, j=PACK)
+    grad_v = grad_out.rearrange("(k p j) w -> k p j w", p=P, j=PACK)
+
+    with ExitStack() as ctx:
+        keep = ctx.enter_context(tc.tile_pool(name="keep", bufs=1))
+        mail = ctx.enter_context(tc.tile_pool(name="mail", bufs=MAIL_BUFS))
+        tree = ctx.enter_context(tc.tile_pool(name="tree", bufs=1))
+        work = ctx.enter_context(tc.tile_pool(name="work", bufs=1))
+        pipe = ctx.enter_context(tc.tile_pool(name="pipe", bufs=2))
+        psum = ctx.enter_context(tc.psum_pool(name="psum", bufs=6))
+
+        gates = []
+        cell = []
+        grad = []
+        hc_rows = []
+        gate_loads = []
+        for k in range(PASSES):
+            gates.append(keep.tile([P, PACK, 3 * H], F32, name="gates%d" % k))
+            cell.append(keep.tile([P, PACK, H], F32, name="cell%d" % k))
+            grad.append(keep.tile([P, PACK, 2 * H], BF16, name="grad%d" % k))
+            hc_rows.append(keep.tile([P, PACK, 2 * H], BF16, name="hc_rows%d" % k))
+            gate_loads.extend([(gates[k], iou_v[k]), (cell[k], cell_v[k]), (grad[k], grad_v[k])])
+        hc_codes = keep.tile([P, PASSES, 2 * H], U32, align_bytes=64)
+        hc_scales = keep.tile([P, PASSES, 2 * H], U8, align_bytes=64)
+
+        for k in range(PASSES):
+            for j in range(PACK):
+                chunk = k * PACK + j
+                x = mail.tile([P, CHILDREN, H], BF16)
+                nc.sync.dma_start(out=x[:], in_=mail_v[k, j])
+                if chunk >= MAIL_BUFS - 1:
+                    dst, src = gate_loads[chunk - (MAIL_BUFS - 1)]
+                    nc.sync.dma_start(out=dst[:], in_=src)
+                sums = tree.tile([P, CHILDREN // 2, H], F32)
+                maxs = tree.tile([P, CHILDREN // 2, H], BF16)
+                nc.vector.tensor_tensor(out=sums[:], in0=x[:, 0:4, :], in1=x[:, 4:8, :], op=ADD)
+                nc.vector.tensor_tensor(out=maxs[:], in0=x[:, 0:4, :], in1=x[:, 4:8, :], op=MAX)
+                nc.vector.tensor_tensor(out=sums[:, 0:2, :], in0=sums[:, 0:2, :], in1=sums[:, 2:4, :], op=ADD)
+                nc.vector.tensor_tensor(out=maxs[:, 0:2, :], in0=maxs[:, 0:2, :], in1=maxs[:, 2:4, :], op=MAX)
+                nc.vector.tensor_tensor(out=hc_rows[k][:, j, 0:H], in0=sums[:, 0, :], in1=sums[:, 1, :], op=ADD)
+                nc.vector.tensor_tensor(out=hc_rows[k][:, j, H : 2 * H], in0=maxs[:, 0, :], in1=maxs[:, 1, :], op=MAX)
+            for half in range(2):
+                cols = slice(half * H, (half + 1) * H)
+                hc_grouped = pipe.tile([P, H, PACK], BF16, align_bytes=64)
+                regroup(nc, hc_grouped[:], hc_rows[k][:, :, cols])
+                nc.vector.quantize_mx(
+                    out=hc_codes[:, k, cols].bitcast(E4M3X4),
+                    scales=hc_scales[:, k, cols],
+                    in_=hc_grouped[:].rearrange("p w j -> p (w j)"),
+                )
+
+        for k in range(PASSES):
+            nc.scalar.activation(out=gates[k][:, :, 0 : 2 * H], in_=gates[k][:, :, 0 : 2 * H], func=TANH, scale=-0.5)
+            nc.scalar.activation(out=gates[k][:, :, 2 * H : 3 * H], in_=gates[k][:, :, 2 * H : 3 * H], func=TANH)
+            nc.scalar.activation(out=cell[k][:], in_=cell[k][:], func=TANH)
+
+        def both_passes(dst, in0, scalar, in1, op0, op1):
+            for k in range(PASSES):
+                nc.vector.scalar_tensor_tensor(out=dst[:, k], in0=in0[k], scalar=scalar, in1=in1[k], op0=op0, op1=op1)
+
+        def halves(t):
+            return [t[:, k] for k in range(PASSES)]
+
+        def multiply_and_store(gate, first_col, rows):
+            grouped = pipe.tile([P, PASSES, P, PACK], BF16, align_bytes=64)
+            codes = pipe.tile([P, PASSES, P], U32, align_bytes=64)
+            scales = pipe.tile([P, PASSES, P], U8, align_bytes=64)
+            for k in range(PASSES):
+                regroup(nc, grouped[:, k], rows[:, k])
+            nc.vector.quantize_mx(
+                out=codes[:].rearrange("p k w -> p (k w)").bitcast(E5M2X4),
+                scales=scales[:].rearrange("p k w -> p (k w)"),
+                in_=grouped[:].rearrange("p k w j -> p (k w j)"),
+            )
+            result = pipe.tile([P, 2 * H], F32)
+            for n in range(2 * H // BANK):
+                n_cols = slice(n * BANK, (n + 1) * BANK)
+                acc = psum.tile([P, BANK], F32)
+                for k in range(PASSES):
+                    nc.tensor.matmul_mx(
+                        out=acc[:],
+                        lhsT=codes[:, k, :].bitcast(E5M2X4),
+                        lhsT_scale=scales[:, k, :],
+                        rhs=hc_codes[:, k, n_cols].bitcast(E4M3X4),
+                        rhs_scale=hc_scales[:, k, n_cols],
+                        start=(k == 0),
+                        stop=(k == PASSES - 1),
+                    )
+                nc.scalar.copy(out=result[:, n_cols], in_=acc[:])
+            first_row = gate * H + first_col
+            nc.sync.dma_start(out=out[first_row : first_row + P, :], in_=result[:])
+
+        for s in range(H // P):
+            lo = s * P
+            t_i = [gates[k][:, :, lo : lo + P] for k in range(PASSES)]
+            t_o = [gates[k][:, :, H + lo : H + lo + P] for k in range(PASSES)]
+            t_u = [gates[k][:, :, 2 * H + lo : 2 * H + lo + P] for k in range(PASSES)]
+            t_c = [cell[k][:, :, lo : lo + P] for k in range(PASSES)]
+            g_h = [grad[k][:, :, lo : lo + P] for k in range(PASSES)]
+            g_c = [grad[k][:, :, H + lo : H + lo + P] for k in range(PASSES)]
+
+            sq_c = work.tile([P, PASSES, PACK, P], F32)
+            sq_u = work.tile([P, PASSES, PACK, P], F32)
+            for k in range(PASSES):
+                nc.scalar.activation(out=sq_c[:, k], in_=t_c[k], func=SQUARE, scale=0.5)
+                nc.scalar.activation(out=sq_u[:, k], in_=t_u[k], func=SQUARE)
+
+            gh_so = work.tile([P, PASSES, PACK, P], F32)
+            both_passes(gh_so, t_o, -1.0, g_h, ADD, MULT)
+            gh_dso = work.tile([P, PASSES, PACK, P], F32)
+            both_passes(gh_dso, t_o, 1.0, halves(gh_so), ADD, MULT)
+            through_h = work.tile([P, PASSES, PACK, P], F32)
+            both_passes(through_h, halves(sq_c), -0.25, halves(gh_so), ADD, MULT)
+            d_o = pipe.tile([P, PASSES, PACK, P], BF16)
+            both_passes(d_o, halves(gh_dso), -0.25, t_c, MULT, MULT)
+            half_dc = work.tile([P, PASSES, PACK, P], F32)
+            both_passes(half_dc, g_c, 0.5, halves(through_h), MULT, ADD)
+            multiply_and_store(1, lo, d_o)
+            dc_si = work.tile([P, PASSES, PACK, P], F32)
+            both_passes(dc_si, t_i, -1.0, halves(half_dc), ADD, MULT)
+            dc_dsi = work.tile([P, PASSES, PACK, P], F32)
+            both_passes(dc_dsi, t_i, 1.0, halves(dc_si), ADD, MULT)
+            d_u = pipe.tile([P, PASSES, PACK, P], BF16)
+            both_passes(d_u, halves(sq_u), -1.0, halves(dc_si), ADD, MULT)
+            d_i = pipe.tile([P, PASSES, PACK, P], BF16)
+            both_passes(d_i, halves(dc_dsi), -0.5, t_u, MULT, MULT)
+            multiply_and_store(2, lo, d_u)
+            multiply_and_store(0, lo, d_i)

@@ -104,12 +104,12 @@ def tile_treelstmcellv2_v_kernel(
         def halves(t):
             return [t[:, k] for k in range(PASSES)]
 
-        def multiply_and_store(gate, first_col, rows):
-            grouped = pipe.tile([P, PASSES, P, PACK], BF16, align_bytes=64)
+        def by_column(views):
+            return [v.rearrange("p j w -> p w j") for v in views]
+
+        def multiply_and_store(gate, first_col, grouped):
             codes = pipe.tile([P, PASSES, P], U32, align_bytes=64)
             scales = pipe.tile([P, PASSES, P], U8, align_bytes=64)
-            for k in range(PASSES):
-                regroup(nc, grouped[:, k], rows[:, k])
             nc.vector.quantize_mx(
                 out=codes[:].rearrange("p k w -> p (k w)").bitcast(E5M2X4),
                 scales=scales[:].rearrange("p k w -> p (k w)"),
@@ -154,8 +154,8 @@ def tile_treelstmcellv2_v_kernel(
             both_passes(gh_dso, t_o, 1.0, halves(gh_so), ADD, MULT)
             through_h = work.tile([P, PASSES, PACK, P], F32)
             both_passes(through_h, halves(sq_c), -0.25, halves(gh_so), ADD, MULT)
-            d_o = pipe.tile([P, PASSES, PACK, P], BF16)
-            both_passes(d_o, halves(gh_dso), -0.25, t_c, MULT, MULT)
+            d_o = pipe.tile([P, PASSES, P, PACK], BF16, align_bytes=64)
+            both_passes(d_o, by_column(halves(gh_dso)), -0.25, by_column(t_c), MULT, MULT)
             half_dc = work.tile([P, PASSES, PACK, P], F32)
             both_passes(half_dc, g_c, 0.5, halves(through_h), MULT, ADD)
             multiply_and_store(1, lo, d_o)
@@ -163,9 +163,9 @@ def tile_treelstmcellv2_v_kernel(
             both_passes(dc_si, t_i, -1.0, halves(half_dc), ADD, MULT)
             dc_dsi = work.tile([P, PASSES, PACK, P], F32)
             both_passes(dc_dsi, t_i, 1.0, halves(dc_si), ADD, MULT)
-            d_u = pipe.tile([P, PASSES, PACK, P], BF16)
-            both_passes(d_u, halves(sq_u), -1.0, halves(dc_si), ADD, MULT)
-            d_i = pipe.tile([P, PASSES, PACK, P], BF16)
-            both_passes(d_i, halves(dc_dsi), -0.5, t_u, MULT, MULT)
+            d_u = pipe.tile([P, PASSES, P, PACK], BF16, align_bytes=64)
+            both_passes(d_u, by_column(halves(sq_u)), -1.0, by_column(halves(dc_si)), ADD, MULT)
+            d_i = pipe.tile([P, PASSES, P, PACK], BF16, align_bytes=64)
+            both_passes(d_i, by_column(halves(dc_dsi)), -0.5, by_column(t_u), MULT, MULT)
             multiply_and_store(2, lo, d_u)
             multiply_and_store(0, lo, d_i)

@@ -1,6 +1,7 @@
 from contextlib import ExitStack
 
 import concourse.mybir as mybir
+from concourse.masks import make_identity
 
 F32 = mybir.dt.float32
 BF16 = mybir.dt.bfloat16
@@ -20,19 +21,19 @@ NODES = 1024
 CHILDREN = 8
 H = 512
 PASSES = NODES // (P * PACK)
+PASS_NODES = P * PACK
 BANK = 512
 RUN = 4
-MAIL_BUFS = 3
+BANKS = 8
+STREAM_BUFS = 5
+SIDE = 2
+PAIRS = CHILDREN // SIDE
+PAIR_NODES = P // PAIRS
+PAIR_TILES = 4
+TWINS = 2
 
 FLOPS = 2 * 3 * H * 2 * H * NODES
 BYTES = 2 * NODES * CHILDREN * H + 4 * NODES * 3 * H + 4 * NODES * H + 2 * NODES * 2 * H + 4 * 3 * H * 2 * H
-
-
-def regroup(nc, grouped, rows):
-    nc.scalar.copy(
-        out=grouped.rearrange("p (b i) j -> p b j i", i=RUN),
-        in_=rows.rearrange("p j (b i) -> p b j i", i=RUN),
-    )
 
 
 def tile_treelstmcellv2_v_kernel(
@@ -43,129 +44,194 @@ def tile_treelstmcellv2_v_kernel(
     iou_v = iou.rearrange("(k p j) w -> k p j w", p=P, j=PACK)
     cell_v = c.rearrange("(k p j) w -> k p j w", p=P, j=PACK)
     grad_v = grad_out.rearrange("(k p j) w -> k p j w", p=P, j=PACK)
+    pair_v = mailbox_h.rearrange("(g t n) (a b) h -> g (n a) t b h", t=PAIR_TILES, n=PAIR_NODES, b=SIDE)
 
     with ExitStack() as ctx:
         keep = ctx.enter_context(tc.tile_pool(name="keep", bufs=1))
-        mail = ctx.enter_context(tc.tile_pool(name="mail", bufs=MAIL_BUFS))
-        tree = ctx.enter_context(tc.tile_pool(name="tree", bufs=1))
-        work = ctx.enter_context(tc.tile_pool(name="work", bufs=1))
+        stream = ctx.enter_context(tc.tile_pool(name="stream", bufs=STREAM_BUFS))
         pipe = ctx.enter_context(tc.tile_pool(name="pipe", bufs=2))
-        psum = ctx.enter_context(tc.psum_pool(name="psum", bufs=6))
+        temp = ctx.enter_context(tc.tile_pool(name="temp", bufs=3))
+        psum = ctx.enter_context(tc.psum_pool(name="psum", bufs=1))
 
-        gates = []
-        cell = []
-        grad = []
-        hc_rows = []
-        gate_loads = []
-        for k in range(PASSES):
-            gates.append(keep.tile([P, PACK, 3 * H], F32, name="gates%d" % k))
-            cell.append(keep.tile([P, PACK, H], F32, name="cell%d" % k))
-            grad.append(keep.tile([P, PACK, 2 * H], BF16, name="grad%d" % k))
-            hc_rows.append(keep.tile([P, PACK, 2 * H], BF16, name="hc_rows%d" % k))
-            gate_loads.extend([(gates[k], iou_v[k]), (cell[k], cell_v[k]), (grad[k], grad_v[k])])
+        ident = keep.tile([P, P], BF16)
+        make_identity(nc, ident[:])
+        pick_f32 = keep.tile([P, PAIR_NODES], F32)
+        nc.vector.tensor_reduce(
+            out=pick_f32[:], in_=ident[:].rearrange("p (n a) -> p n a", a=PAIRS), axis=mybir.AxisListType.X, op=ADD
+        )
+        pick = keep.tile([P, PAIR_NODES], BF16)
+        nc.vector.tensor_copy(out=pick[:], in_=pick_f32[:])
+
         hc_codes = keep.tile([P, PASSES, 2 * H], U32, align_bytes=64)
         hc_scales = keep.tile([P, PASSES, 2 * H], U8, align_bytes=64)
+        d_codes = keep.tile([P, PASSES, 3, H], U32, align_bytes=64)
+        d_scales = keep.tile([P, PASSES, 3, H], U8, align_bytes=64)
+
+        t_i = []
+        t_o = []
+        t_u = []
+        t_c = []
+        grad = []
+        max_rows = []
+        for k in range(PASSES):
+            t_i.append(keep.tile([P, PACK, H], F32, name="t_i%d" % k))
+            t_o.append(keep.tile([P, PACK, H], F32, name="t_o%d" % k))
+            t_u.append(keep.tile([P, PACK, H], F32, name="t_u%d" % k))
+            t_c.append(keep.tile([P, PACK, H], F32, name="t_c%d" % k))
+            grad.append(keep.tile([P, PACK, 2 * H], BF16, name="grad%d" % k))
+            max_rows.append(keep.tile([P, PACK, H], BF16, name="max_rows%d" % k))
+
+        def load_gate_inputs(k):
+            nc.sync.dma_start(out=t_o[k][:], in_=iou_v[k][:, :, H : 2 * H])
+            nc.sync.dma_start(out=grad[k][:], in_=grad_v[k])
+            nc.sync.dma_start(out=t_c[k][:], in_=cell_v[k])
+            nc.sync.dma_start(out=t_i[k][:], in_=iou_v[k][:, :, 0:H])
+            nc.sync.dma_start(out=t_u[k][:], in_=iou_v[k][:, :, 2 * H : 3 * H])
+            nc.scalar.activation(out=t_o[k][:], in_=t_o[k][:], func=TANH, scale=-0.5)
+            nc.scalar.activation(out=t_c[k][:], in_=t_c[k][:], func=TANH)
+            nc.scalar.activation(out=t_i[k][:], in_=t_i[k][:], func=TANH, scale=-0.5)
+            nc.scalar.activation(out=t_u[k][:], in_=t_u[k][:], func=TANH)
+
+        def quantise_hc(k, half, hc_grouped):
+            cols = slice(half * H, (half + 1) * H)
+            nc.vector.quantize_mx(
+                out=hc_codes[:, k, cols].bitcast(E4M3X4),
+                scales=hc_scales[:, k, cols],
+                in_=hc_grouped[:].rearrange("p w j -> p (w j)"),
+            )
+
+        for k in range(PASSES):
+            load_gate_inputs(k)
+
+        for k in range(PASSES):
+            sum_t = [psum.tile([P, PASS_NODES], F32, name="sum_t%d" % q, tag="bank", bufs=BANKS - 1) for q in range(H // P)]
+            loads = PASS_NODES // (PAIR_TILES * PAIR_NODES)
+            for g in range(loads):
+                pairs = stream.tile([P, PAIR_TILES, SIDE, H], BF16, tag="stream")
+                nc.sync.dma_start(out=pairs[:], in_=pair_v[k * loads + g])
+                for t in range(PAIR_TILES):
+                    first = (g * PAIR_TILES + t) * PAIR_NODES
+                    for q in range(H // P):
+                        for b in range(SIDE):
+                            nc.tensor.matmul(
+                                out=sum_t[q][:, first : first + PAIR_NODES],
+                                lhsT=pairs[:, t, b, q * P : (q + 1) * P],
+                                rhs=pick[:],
+                                start=(b == 0),
+                                stop=(b == SIDE - 1),
+                            )
+            sum_t_rows = pipe.tile([P, H // P, PACK, P], BF16, bufs=1)
+            for q in range(H // P):
+                nc.scalar.copy(out=sum_t_rows[:, q], in_=sum_t[q][:].rearrange("h (p j) -> h j p", j=PACK))
+            sum_grouped = pipe.tile([P, H, PACK], BF16, align_bytes=64, tag="hc_grouped")
+            per_bank = 2
+            for half in range(H // (per_bank * P)):
+                back = psum.tile([P, PACK, per_bank * P], BF16)
+                for j in range(PACK):
+                    for r in range(per_bank):
+                        nc.tensor.transpose(
+                            out=back[:, j, r * P : (r + 1) * P],
+                            in_=sum_t_rows[:, half * per_bank + r, j, :],
+                            identity=ident[:],
+                        )
+                w_cols = slice(half * per_bank * P, (half + 1) * per_bank * P)
+                nc.scalar.copy(out=sum_grouped[:, w_cols, :], in_=back[:].rearrange("p j w -> p w j"))
+            quantise_hc(k, 0, sum_grouped)
 
         for k in range(PASSES):
             for j in range(PACK):
-                chunk = k * PACK + j
-                x = mail.tile([P, CHILDREN, H], BF16)
+                x = stream.tile([P, CHILDREN, H], BF16, tag="stream")
                 nc.sync.dma_start(out=x[:], in_=mail_v[k, j])
-                if chunk >= MAIL_BUFS - 1:
-                    dst, src = gate_loads[chunk - (MAIL_BUFS - 1)]
-                    nc.sync.dma_start(out=dst[:], in_=src)
-                sums = tree.tile([P, CHILDREN // 2, H], F32)
-                maxs = tree.tile([P, CHILDREN // 2, H], BF16)
-                nc.vector.tensor_tensor(out=sums[:], in0=x[:, 0:4, :], in1=x[:, 4:8, :], op=ADD)
+                maxs = pipe.tile([P, CHILDREN // 2, H], BF16)
                 nc.vector.tensor_tensor(out=maxs[:], in0=x[:, 0:4, :], in1=x[:, 4:8, :], op=MAX)
-                nc.vector.tensor_tensor(out=sums[:, 0:2, :], in0=sums[:, 0:2, :], in1=sums[:, 2:4, :], op=ADD)
                 nc.vector.tensor_tensor(out=maxs[:, 0:2, :], in0=maxs[:, 0:2, :], in1=maxs[:, 2:4, :], op=MAX)
-                nc.vector.tensor_tensor(out=hc_rows[k][:, j, 0:H], in0=sums[:, 0, :], in1=sums[:, 1, :], op=ADD)
-                nc.vector.tensor_tensor(out=hc_rows[k][:, j, H : 2 * H], in0=maxs[:, 0, :], in1=maxs[:, 1, :], op=MAX)
-            for half in range(2):
-                cols = slice(half * H, (half + 1) * H)
-                hc_grouped = pipe.tile([P, H, PACK], BF16, align_bytes=64)
-                regroup(nc, hc_grouped[:], hc_rows[k][:, :, cols])
-                nc.vector.quantize_mx(
-                    out=hc_codes[:, k, cols].bitcast(E4M3X4),
-                    scales=hc_scales[:, k, cols],
-                    in_=hc_grouped[:].rearrange("p w j -> p (w j)"),
-                )
+                nc.vector.tensor_tensor(out=max_rows[k][:, j, :], in0=maxs[:, 0, :], in1=maxs[:, 1, :], op=MAX)
+            max_grouped = pipe.tile([P, H, PACK], BF16, align_bytes=64, tag="hc_grouped")
+            nc.scalar.copy(
+                out=max_grouped[:].rearrange("p (b i) j -> p b j i", i=RUN),
+                in_=max_rows[k][:].rearrange("p j (b i) -> p b j i", i=RUN),
+            )
+            quantise_hc(k, 1, max_grouped)
 
-        for k in range(PASSES):
-            nc.scalar.activation(out=gates[k][:, :, 0 : 2 * H], in_=gates[k][:, :, 0 : 2 * H], func=TANH, scale=-0.5)
-            nc.scalar.activation(out=gates[k][:, :, 2 * H : 3 * H], in_=gates[k][:, :, 2 * H : 3 * H], func=TANH)
-            nc.scalar.activation(out=cell[k][:], in_=cell[k][:], func=TANH)
+        def column_blocks(rows, lo):
+            return [rows[:, :, lo + w * P : lo + (w + 1) * P] for w in range(TWINS)]
 
-        def both_passes(dst, in0, scalar, in1, op0, op1):
-            for k in range(PASSES):
-                nc.vector.scalar_tensor_tensor(out=dst[:, k], in0=in0[k], scalar=scalar, in1=in1[k], op0=op0, op1=op1)
-
-        def halves(t):
-            return [t[:, k] for k in range(PASSES)]
+        def blocks(t):
+            return [t[:, w] for w in range(TWINS)]
 
         def by_column(views):
-            return [v.rearrange("p j w -> p w j") for v in views]
+            return [v.rearrange("p j c -> p c j") for v in views]
 
-        def multiply_and_store(gate, first_col, grouped):
-            codes = pipe.tile([P, PASSES, P], U32, align_bytes=64)
-            scales = pipe.tile([P, PASSES, P], U8, align_bytes=64)
+        def product(dst, in0, scalar, in1, op0, op1):
+            for w in range(TWINS):
+                nc.vector.scalar_tensor_tensor(out=dst[:, w], in0=in0[w], scalar=scalar, in1=in1[w], op0=op0, op1=op1)
+
+        def quantise_gate(k, gate, lo, grouped):
             nc.vector.quantize_mx(
-                out=codes[:].rearrange("p k w -> p (k w)").bitcast(E5M2X4),
-                scales=scales[:].rearrange("p k w -> p (k w)"),
-                in_=grouped[:].rearrange("p k w j -> p (k w j)"),
+                out=d_codes[:, k, gate, lo : lo + TWINS * P].bitcast(E5M2X4),
+                scales=d_scales[:, k, gate, lo : lo + TWINS * P],
+                in_=grouped[:].rearrange("p w c j -> p (w c j)"),
             )
-            result = pipe.tile([P, 2 * H], F32)
-            for n in range(2 * H // BANK):
-                n_cols = slice(n * BANK, (n + 1) * BANK)
-                acc = psum.tile([P, BANK], F32)
-                for k in range(PASSES):
-                    nc.tensor.matmul_mx(
-                        out=acc[:],
-                        lhsT=codes[:, k, :].bitcast(E5M2X4),
-                        lhsT_scale=scales[:, k, :],
-                        rhs=hc_codes[:, k, n_cols].bitcast(E4M3X4),
-                        rhs_scale=hc_scales[:, k, n_cols],
-                        start=(k == 0),
-                        stop=(k == PASSES - 1),
-                    )
-                nc.scalar.copy(out=result[:, n_cols], in_=acc[:])
-            first_row = gate * H + first_col
-            nc.sync.dma_start(out=out[first_row : first_row + P, :], in_=result[:])
 
-        for s in range(H // P):
-            lo = s * P
-            t_i = [gates[k][:, :, lo : lo + P] for k in range(PASSES)]
-            t_o = [gates[k][:, :, H + lo : H + lo + P] for k in range(PASSES)]
-            t_u = [gates[k][:, :, 2 * H + lo : 2 * H + lo + P] for k in range(PASSES)]
-            t_c = [cell[k][:, :, lo : lo + P] for k in range(PASSES)]
-            g_h = [grad[k][:, :, lo : lo + P] for k in range(PASSES)]
-            g_c = [grad[k][:, :, H + lo : H + lo + P] for k in range(PASSES)]
+        block = [P, TWINS, PACK, P]
+        grouped_block = [P, TWINS, P, PACK]
+        for k in range(PASSES):
+            for lo in range(0, H, TWINS * P):
+                tanh_i = column_blocks(t_i[k], lo)
+                tanh_o = column_blocks(t_o[k], lo)
+                tanh_u = column_blocks(t_u[k], lo)
+                tanh_c = column_blocks(t_c[k], lo)
+                g_h = column_blocks(grad[k], lo)
+                g_c = column_blocks(grad[k], H + lo)
+                sq_c = pipe.tile(block, F32)
+                sq_u = pipe.tile(block, F32)
+                for w in range(TWINS):
+                    nc.scalar.activation(out=sq_c[:, w], in_=tanh_c[w], func=SQUARE, scale=0.5)
+                for w in range(TWINS):
+                    nc.scalar.activation(out=sq_u[:, w], in_=tanh_u[w], func=SQUARE)
 
-            sq_c = work.tile([P, PASSES, PACK, P], F32)
-            sq_u = work.tile([P, PASSES, PACK, P], F32)
-            for k in range(PASSES):
-                nc.scalar.activation(out=sq_c[:, k], in_=t_c[k], func=SQUARE, scale=0.5)
-                nc.scalar.activation(out=sq_u[:, k], in_=t_u[k], func=SQUARE)
+                gh_so = temp.tile(block, F32, tag="temp")
+                product(gh_so, tanh_o, -1.0, g_h, ADD, MULT)
+                gh_dso = temp.tile(block, F32, tag="temp")
+                product(gh_dso, tanh_o, 1.0, blocks(gh_so), ADD, MULT)
+                through_h = temp.tile(block, F32, tag="temp")
+                product(through_h, blocks(sq_c), -0.25, blocks(gh_so), ADD, MULT)
+                d_o = pipe.tile(grouped_block, BF16, align_bytes=64)
+                product(d_o, by_column(blocks(gh_dso)), -0.25, by_column(tanh_c), MULT, MULT)
+                half_dc = temp.tile(block, F32, tag="temp")
+                product(half_dc, g_c, 0.5, blocks(through_h), MULT, ADD)
+                quantise_gate(k, 1, lo, d_o)
+                dc_si = temp.tile(block, F32, tag="temp")
+                product(dc_si, tanh_i, -1.0, blocks(half_dc), ADD, MULT)
+                dc_dsi = temp.tile(block, F32, tag="temp")
+                product(dc_dsi, tanh_i, 1.0, blocks(dc_si), ADD, MULT)
+                d_u = pipe.tile(grouped_block, BF16, align_bytes=64)
+                product(d_u, by_column(blocks(sq_u)), -1.0, by_column(blocks(dc_si)), ADD, MULT)
+                d_i = pipe.tile(grouped_block, BF16, align_bytes=64)
+                product(d_i, by_column(blocks(dc_dsi)), -0.5, by_column(tanh_u), MULT, MULT)
+                quantise_gate(k, 2, lo, d_u)
+                quantise_gate(k, 0, lo, d_i)
 
-            gh_so = work.tile([P, PASSES, PACK, P], F32)
-            both_passes(gh_so, t_o, -1.0, g_h, ADD, MULT)
-            gh_dso = work.tile([P, PASSES, PACK, P], F32)
-            both_passes(gh_dso, t_o, 1.0, halves(gh_so), ADD, MULT)
-            through_h = work.tile([P, PASSES, PACK, P], F32)
-            both_passes(through_h, halves(sq_c), -0.25, halves(gh_so), ADD, MULT)
-            d_o = pipe.tile([P, PASSES, P, PACK], BF16, align_bytes=64)
-            both_passes(d_o, by_column(halves(gh_dso)), -0.25, by_column(t_c), MULT, MULT)
-            half_dc = work.tile([P, PASSES, PACK, P], F32)
-            both_passes(half_dc, g_c, 0.5, halves(through_h), MULT, ADD)
-            multiply_and_store(1, lo, d_o)
-            dc_si = work.tile([P, PASSES, PACK, P], F32)
-            both_passes(dc_si, t_i, -1.0, halves(half_dc), ADD, MULT)
-            dc_dsi = work.tile([P, PASSES, PACK, P], F32)
-            both_passes(dc_dsi, t_i, 1.0, halves(dc_si), ADD, MULT)
-            d_u = pipe.tile([P, PASSES, P, PACK], BF16, align_bytes=64)
-            both_passes(d_u, by_column(halves(sq_u)), -1.0, by_column(halves(dc_si)), ADD, MULT)
-            d_i = pipe.tile([P, PASSES, P, PACK], BF16, align_bytes=64)
-            both_passes(d_i, by_column(halves(dc_dsi)), -0.5, by_column(t_u), MULT, MULT)
-            multiply_and_store(2, lo, d_u)
-            multiply_and_store(0, lo, d_i)
+        out_v = out.rearrange("(g m p) w -> g m p w", m=H // P, p=P)
+        for n in range(2 * H // BANK):
+            n_cols = slice(n * BANK, (n + 1) * BANK)
+            for gate in range(3):
+                results = stream.tile([P, H // P, BANK], F32, tag="stream")
+                for m in range(H // P):
+                    m_cols = slice(m * P, (m + 1) * P)
+                    acc = psum.tile([P, BANK], F32, tag="bank", bufs=BANKS - 1)
+                    for k in range(PASSES):
+                        nc.tensor.matmul_mx(
+                            out=acc[:],
+                            lhsT=d_codes[:, k, gate, m_cols].bitcast(E5M2X4),
+                            lhsT_scale=d_scales[:, k, gate, m_cols],
+                            rhs=hc_codes[:, k, n_cols].bitcast(E4M3X4),
+                            rhs_scale=hc_scales[:, k, n_cols],
+                            start=(k == 0),
+                            stop=(k == PASSES - 1),
+                        )
+                    if n == 1 and m % 2 == 1:
+                        nc.vector.tensor_copy(out=results[:, m], in_=acc[:])
+                    else:
+                        nc.scalar.copy(out=results[:, m], in_=acc[:])
+                    nc.sync.dma_start(out=out_v[gate, m][:, n_cols], in_=results[:, m])

@@ -23,13 +23,15 @@ H = 512
 PASSES = NODES // (P * PACK)
 PASS_NODES = P * PACK
 BANK = 512
-RUN = 4
 BANKS = 8
-STREAM_BUFS = 5
+H_BLOCKS = H // P
 SIDE = 2
 PAIRS = CHILDREN // SIDE
 PAIR_NODES = P // PAIRS
 PAIR_TILES = 4
+LOADS = PASS_NODES // (PAIR_TILES * PAIR_NODES)
+OCTET = PAIR_NODES // PACK
+PER_BANK = 2
 TWINS = 2
 
 FLOPS = 2 * 3 * H * 2 * H * NODES
@@ -40,7 +42,6 @@ def tile_treelstmcellv2_v_kernel(
     tc, mailbox_h, mailbox_c, U_iou_w, b_iou, U_f_w, U_f_b, iou, c, grad_out, out
 ):
     nc = tc.nc
-    mail_v = mailbox_h.rearrange("(k p j) ch h -> k j p ch h", p=P, j=PACK)
     iou_v = iou.rearrange("(k p j) w -> k p j w", p=P, j=PACK)
     cell_v = c.rearrange("(k p j) w -> k p j w", p=P, j=PACK)
     grad_v = grad_out.rearrange("(k p j) w -> k p j w", p=P, j=PACK)
@@ -48,7 +49,7 @@ def tile_treelstmcellv2_v_kernel(
 
     with ExitStack() as ctx:
         keep = ctx.enter_context(tc.tile_pool(name="keep", bufs=1))
-        stream = ctx.enter_context(tc.tile_pool(name="stream", bufs=STREAM_BUFS))
+        stream = ctx.enter_context(tc.tile_pool(name="stream", bufs=3))
         pipe = ctx.enter_context(tc.tile_pool(name="pipe", bufs=2))
         temp = ctx.enter_context(tc.tile_pool(name="temp", bufs=3))
         psum = ctx.enter_context(tc.psum_pool(name="psum", bufs=1))
@@ -61,6 +62,11 @@ def tile_treelstmcellv2_v_kernel(
         )
         pick = keep.tile([P, PAIR_NODES], BF16)
         nc.vector.tensor_copy(out=pick[:], in_=pick_f32[:])
+        sort = keep.tile([P, P], BF16)
+        nc.vector.tensor_copy(
+            out=sort[:].rearrange("p (a j r) -> p a j r", a=PAIRS, j=PACK),
+            in_=ident[:].rearrange("p (r j a) -> p a j r", a=PAIRS, j=PACK),
+        )
 
         hc_codes = keep.tile([P, PASSES, 2 * H], U32, align_bytes=64)
         hc_scales = keep.tile([P, PASSES, 2 * H], U8, align_bytes=64)
@@ -72,14 +78,12 @@ def tile_treelstmcellv2_v_kernel(
         t_u = []
         t_c = []
         grad = []
-        max_rows = []
         for k in range(PASSES):
             t_i.append(keep.tile([P, PACK, H], F32, name="t_i%d" % k))
             t_o.append(keep.tile([P, PACK, H], F32, name="t_o%d" % k))
             t_u.append(keep.tile([P, PACK, H], F32, name="t_u%d" % k))
             t_c.append(keep.tile([P, PACK, H], F32, name="t_c%d" % k))
             grad.append(keep.tile([P, PACK, 2 * H], BF16, name="grad%d" % k))
-            max_rows.append(keep.tile([P, PACK, H], BF16, name="max_rows%d" % k))
 
         def load_gate_inputs(k):
             nc.sync.dma_start(out=t_o[k][:], in_=iou_v[k][:, :, H : 2 * H])
@@ -92,26 +96,38 @@ def tile_treelstmcellv2_v_kernel(
             nc.scalar.activation(out=t_i[k][:], in_=t_i[k][:], func=TANH, scale=-0.5)
             nc.scalar.activation(out=t_u[k][:], in_=t_u[k][:], func=TANH)
 
-        def quantise_hc(k, half, hc_grouped):
+        def quantise_hc(k, half, by_hidden):
+            grouped = pipe.tile([P, H, PACK], BF16, align_bytes=64)
+            for piece in range(H_BLOCKS // PER_BANK):
+                back = psum.tile([P, PACK, PER_BANK * P], BF16)
+                for j in range(PACK):
+                    for r in range(PER_BANK):
+                        nc.tensor.transpose(
+                            out=back[:, j, r * P : (r + 1) * P],
+                            in_=by_hidden[:, piece * PER_BANK + r, j, :],
+                            identity=ident[:],
+                        )
+                w_cols = slice(piece * PER_BANK * P, (piece + 1) * PER_BANK * P)
+                nc.scalar.copy(out=grouped[:, w_cols, :], in_=back[:].rearrange("p j w -> p w j"))
             cols = slice(half * H, (half + 1) * H)
             nc.vector.quantize_mx(
                 out=hc_codes[:, k, cols].bitcast(E4M3X4),
                 scales=hc_scales[:, k, cols],
-                in_=hc_grouped[:].rearrange("p w j -> p (w j)"),
+                in_=grouped[:].rearrange("p w j -> p (w j)"),
             )
 
         for k in range(PASSES):
             load_gate_inputs(k)
-
-        for k in range(PASSES):
-            sum_t = [psum.tile([P, PASS_NODES], F32, name="sum_t%d" % q, tag="bank", bufs=BANKS - 1) for q in range(H // P)]
-            loads = PASS_NODES // (PAIR_TILES * PAIR_NODES)
-            for g in range(loads):
-                pairs = stream.tile([P, PAIR_TILES, SIDE, H], BF16, tag="stream")
-                nc.sync.dma_start(out=pairs[:], in_=pair_v[k * loads + g])
-                for t in range(PAIR_TILES):
-                    first = (g * PAIR_TILES + t) * PAIR_NODES
-                    for q in range(H // P):
+            sum_t = [psum.tile([P, PASS_NODES], F32, name="sum_t%d" % q, tag="bank", bufs=BANKS - 1) for q in range(H_BLOCKS)]
+            pair_max_t = pipe.tile([P, H_BLOCKS, PAIRS * PACK, P], BF16, bufs=1)
+            for g in range(LOADS):
+                pairs = stream.tile([P, PAIR_TILES, SIDE, H], BF16)
+                nc.sync.dma_start(out=pairs[:], in_=pair_v[k * LOADS + g])
+                pair_max = pipe.tile([P, PAIR_TILES, H], BF16)
+                nc.vector.tensor_tensor(out=pair_max[:], in0=pairs[:, :, 0, :], in1=pairs[:, :, 1, :], op=MAX)
+                for q in range(H_BLOCKS):
+                    for t in range(PAIR_TILES):
+                        first = (g * PAIR_TILES + t) * PAIR_NODES
                         for b in range(SIDE):
                             nc.tensor.matmul(
                                 out=sum_t[q][:, first : first + PAIR_NODES],
@@ -120,38 +136,27 @@ def tile_treelstmcellv2_v_kernel(
                                 start=(b == 0),
                                 stop=(b == SIDE - 1),
                             )
-            sum_t_rows = pipe.tile([P, H // P, PACK, P], BF16, bufs=1)
-            for q in range(H // P):
-                nc.scalar.copy(out=sum_t_rows[:, q], in_=sum_t[q][:].rearrange("h (p j) -> h j p", j=PACK))
-            sum_grouped = pipe.tile([P, H, PACK], BF16, align_bytes=64, tag="hc_grouped")
-            per_bank = 2
-            for half in range(H // (per_bank * P)):
-                back = psum.tile([P, PACK, per_bank * P], BF16)
-                for j in range(PACK):
-                    for r in range(per_bank):
-                        nc.tensor.transpose(
-                            out=back[:, j, r * P : (r + 1) * P],
-                            in_=sum_t_rows[:, half * per_bank + r, j, :],
-                            identity=ident[:],
+                for piece in range(H_BLOCKS // PER_BANK):
+                    turned = psum.tile([P, PER_BANK, PAIR_TILES, P], BF16, tag="bank", bufs=BANKS - 1)
+                    for r in range(PER_BANK):
+                        q = piece * PER_BANK + r
+                        for t in range(PAIR_TILES):
+                            nc.tensor.transpose(out=turned[:, r, t, :], in_=pair_max[:, t, q * P : (q + 1) * P], identity=sort[:])
+                        p_cols = slice(g * PAIR_TILES * OCTET, (g + 1) * PAIR_TILES * OCTET)
+                        nc.scalar.copy(
+                            out=pair_max_t[:, q, :, p_cols].rearrange("h e (t r) -> h e t r", r=OCTET),
+                            in_=turned[:, r].rearrange("h t (e r) -> h e t r", r=OCTET),
                         )
-                w_cols = slice(half * per_bank * P, (half + 1) * per_bank * P)
-                nc.scalar.copy(out=sum_grouped[:, w_cols, :], in_=back[:].rearrange("p j w -> p w j"))
-            quantise_hc(k, 0, sum_grouped)
-
-        for k in range(PASSES):
-            for j in range(PACK):
-                x = stream.tile([P, CHILDREN, H], BF16, tag="stream")
-                nc.sync.dma_start(out=x[:], in_=mail_v[k, j])
-                maxs = pipe.tile([P, CHILDREN // 2, H], BF16)
-                nc.vector.tensor_tensor(out=maxs[:], in0=x[:, 0:4, :], in1=x[:, 4:8, :], op=MAX)
-                nc.vector.tensor_tensor(out=maxs[:, 0:2, :], in0=maxs[:, 0:2, :], in1=maxs[:, 2:4, :], op=MAX)
-                nc.vector.tensor_tensor(out=max_rows[k][:, j, :], in0=maxs[:, 0, :], in1=maxs[:, 1, :], op=MAX)
-            max_grouped = pipe.tile([P, H, PACK], BF16, align_bytes=64, tag="hc_grouped")
-            nc.scalar.copy(
-                out=max_grouped[:].rearrange("p (b i) j -> p b j i", i=RUN),
-                in_=max_rows[k][:].rearrange("p j (b i) -> p b j i", i=RUN),
-            )
-            quantise_hc(k, 1, max_grouped)
+            sum_by_hidden = pipe.tile([P, H_BLOCKS, PACK, P], BF16, tag="by_hidden")
+            for q in range(H_BLOCKS):
+                nc.scalar.copy(out=sum_by_hidden[:, q], in_=sum_t[q][:].rearrange("h (p j) -> h j p", j=PACK))
+            quantise_hc(k, 0, sum_by_hidden)
+            e_half = PAIRS * PACK // 2
+            two_max_t = pipe.tile([P, H_BLOCKS, e_half, P], BF16, bufs=1)
+            nc.vector.tensor_tensor(out=two_max_t[:], in0=pair_max_t[:, :, 0:e_half, :], in1=pair_max_t[:, :, e_half:, :], op=MAX)
+            max_by_hidden = pipe.tile([P, H_BLOCKS, PACK, P], BF16, tag="by_hidden")
+            nc.vector.tensor_tensor(out=max_by_hidden[:], in0=two_max_t[:, :, 0:PACK, :], in1=two_max_t[:, :, PACK:, :], op=MAX)
+            quantise_hc(k, 1, max_by_hidden)
 
         def column_blocks(rows, lo):
             return [rows[:, :, lo + w * P : lo + (w + 1) * P] for w in range(TWINS)]
@@ -173,9 +178,29 @@ def tile_treelstmcellv2_v_kernel(
                 in_=grouped[:].rearrange("p w c j -> p (w c j)"),
             )
 
+        def multiply_and_store(gate, lo):
+            for m in range(lo, lo + TWINS * P, P):
+                result = pipe.tile([P, 2 * H], F32, bufs=3)
+                for n in range(2 * H // BANK):
+                    n_cols = slice(n * BANK, (n + 1) * BANK)
+                    acc = psum.tile([P, BANK], F32, tag="bank", bufs=BANKS - 1)
+                    for k in range(PASSES):
+                        nc.tensor.matmul_mx(
+                            out=acc[:],
+                            lhsT=d_codes[:, k, gate, m : m + P].bitcast(E5M2X4),
+                            lhsT_scale=d_scales[:, k, gate, m : m + P],
+                            rhs=hc_codes[:, k, n_cols].bitcast(E4M3X4),
+                            rhs_scale=hc_scales[:, k, n_cols],
+                            start=(k == 0),
+                            stop=(k == PASSES - 1),
+                        )
+                    nc.scalar.copy(out=result[:, n_cols], in_=acc[:])
+                nc.sync.dma_start(out=out[gate * H + m : gate * H + m + P, :], in_=result[:])
+
         block = [P, TWINS, PACK, P]
         grouped_block = [P, TWINS, P, PACK]
         for k in range(PASSES):
+            last = k == PASSES - 1
             for lo in range(0, H, TWINS * P):
                 tanh_i = column_blocks(t_i[k], lo)
                 tanh_o = column_blocks(t_o[k], lo)
@@ -201,6 +226,8 @@ def tile_treelstmcellv2_v_kernel(
                 half_dc = temp.tile(block, F32, tag="temp")
                 product(half_dc, g_c, 0.5, blocks(through_h), MULT, ADD)
                 quantise_gate(k, 1, lo, d_o)
+                if last:
+                    multiply_and_store(1, lo)
                 dc_si = temp.tile(block, F32, tag="temp")
                 product(dc_si, tanh_i, -1.0, blocks(half_dc), ADD, MULT)
                 dc_dsi = temp.tile(block, F32, tag="temp")
@@ -210,28 +237,8 @@ def tile_treelstmcellv2_v_kernel(
                 d_i = pipe.tile(grouped_block, BF16, align_bytes=64)
                 product(d_i, by_column(blocks(dc_dsi)), -0.5, by_column(tanh_u), MULT, MULT)
                 quantise_gate(k, 2, lo, d_u)
+                if last:
+                    multiply_and_store(2, lo)
                 quantise_gate(k, 0, lo, d_i)
-
-        out_v = out.rearrange("(g m p) w -> g m p w", m=H // P, p=P)
-        for n in range(2 * H // BANK):
-            n_cols = slice(n * BANK, (n + 1) * BANK)
-            for gate in range(3):
-                results = stream.tile([P, H // P, BANK], F32, tag="stream")
-                for m in range(H // P):
-                    m_cols = slice(m * P, (m + 1) * P)
-                    acc = psum.tile([P, BANK], F32, tag="bank", bufs=BANKS - 1)
-                    for k in range(PASSES):
-                        nc.tensor.matmul_mx(
-                            out=acc[:],
-                            lhsT=d_codes[:, k, gate, m_cols].bitcast(E5M2X4),
-                            lhsT_scale=d_scales[:, k, gate, m_cols],
-                            rhs=hc_codes[:, k, n_cols].bitcast(E4M3X4),
-                            rhs_scale=hc_scales[:, k, n_cols],
-                            start=(k == 0),
-                            stop=(k == PASSES - 1),
-                        )
-                    if n == 1 and m % 2 == 1:
-                        nc.vector.tensor_copy(out=results[:, m], in_=acc[:])
-                    else:
-                        nc.scalar.copy(out=results[:, m], in_=acc[:])
-                    nc.sync.dma_start(out=out_v[gate, m][:, n_cols], in_=results[:, m])
+                if last:
+                    multiply_and_store(0, lo)

@@ -31,8 +31,10 @@ PAIR_NODES = P // PAIRS
 PAIR_TILES = 4
 LOADS = PASS_NODES // (PAIR_TILES * PAIR_NODES)
 OCTET = PAIR_NODES // PACK
-PER_BANK = 2
+WORD = 2
+W_BLOCKS = H // (WORD * P)
 TWINS = 2
+UNIT = TWINS * P
 
 FLOPS = 2 * 3 * H * 2 * H * NODES
 BYTES = 2 * NODES * CHILDREN * H + 4 * NODES * 3 * H + 4 * NODES * H + 2 * NODES * 2 * H + 4 * 3 * H * 2 * H
@@ -62,10 +64,12 @@ def tile_treelstmcellv2_v_kernel(
         )
         pick = keep.tile([P, PAIR_NODES], BF16)
         nc.vector.tensor_copy(out=pick[:], in_=pick_f32[:])
-        sort = keep.tile([P, P], BF16)
+        ident_f32 = keep.tile([P, P], F32)
+        make_identity(nc, ident_f32[:])
+        sort = keep.tile([P, P], F32)
         nc.vector.tensor_copy(
             out=sort[:].rearrange("p (a j r) -> p a j r", a=PAIRS, j=PACK),
-            in_=ident[:].rearrange("p (r j a) -> p a j r", a=PAIRS, j=PACK),
+            in_=ident_f32[:].rearrange("p (r j a) -> p a j r", a=PAIRS, j=PACK),
         )
 
         hc_codes = keep.tile([P, PASSES, 2 * H], U32, align_bytes=64)
@@ -85,30 +89,33 @@ def tile_treelstmcellv2_v_kernel(
             t_c.append(keep.tile([P, PACK, H], F32, name="t_c%d" % k))
             grad.append(keep.tile([P, PACK, 2 * H], BF16, name="grad%d" % k))
 
-        def load_gate_inputs(k):
-            nc.sync.dma_start(out=t_o[k][:], in_=iou_v[k][:, :, H : 2 * H])
-            nc.sync.dma_start(out=grad[k][:], in_=grad_v[k])
-            nc.sync.dma_start(out=t_c[k][:], in_=cell_v[k])
-            nc.sync.dma_start(out=t_i[k][:], in_=iou_v[k][:, :, 0:H])
-            nc.sync.dma_start(out=t_u[k][:], in_=iou_v[k][:, :, 2 * H : 3 * H])
-            nc.scalar.activation(out=t_o[k][:], in_=t_o[k][:], func=TANH, scale=-0.5)
-            nc.scalar.activation(out=t_c[k][:], in_=t_c[k][:], func=TANH)
-            nc.scalar.activation(out=t_i[k][:], in_=t_i[k][:], func=TANH, scale=-0.5)
-            nc.scalar.activation(out=t_u[k][:], in_=t_u[k][:], func=TANH)
+        def load_gate_inputs(k, lo):
+            cols = slice(lo, lo + UNIT)
+            nc.sync.dma_start(out=t_o[k][:, :, cols], in_=iou_v[k][:, :, H + lo : H + lo + UNIT])
+            nc.sync.dma_start(out=grad[k][:, :, cols], in_=grad_v[k][:, :, cols])
+            nc.sync.dma_start(out=t_c[k][:, :, cols], in_=cell_v[k][:, :, cols])
+            nc.sync.dma_start(out=grad[k][:, :, H + lo : H + lo + UNIT], in_=grad_v[k][:, :, H + lo : H + lo + UNIT])
+            nc.sync.dma_start(out=t_i[k][:, :, cols], in_=iou_v[k][:, :, cols])
+            nc.sync.dma_start(out=t_u[k][:, :, cols], in_=iou_v[k][:, :, 2 * H + lo : 2 * H + lo + UNIT])
+            nc.scalar.activation(out=t_o[k][:, :, cols], in_=t_o[k][:, :, cols], func=TANH, scale=-0.5)
+            nc.scalar.activation(out=t_c[k][:, :, cols], in_=t_c[k][:, :, cols], func=TANH)
+            nc.scalar.activation(out=t_i[k][:, :, cols], in_=t_i[k][:, :, cols], func=TANH, scale=-0.5)
+            nc.scalar.activation(out=t_u[k][:, :, cols], in_=t_u[k][:, :, cols], func=TANH)
 
-        def quantise_hc(k, half, by_hidden):
+        def quantise_hc(k, half, by_hidden, identity):
             grouped = pipe.tile([P, H, PACK], BF16, align_bytes=64)
-            for piece in range(H_BLOCKS // PER_BANK):
-                back = psum.tile([P, PACK, PER_BANK * P], BF16)
+            per_bank = by_hidden.shape[1] // W_BLOCKS
+            for piece in range(W_BLOCKS):
+                back = psum.tile([P, PACK, per_bank * P], by_hidden.dtype, tag="back")
                 for j in range(PACK):
-                    for r in range(PER_BANK):
+                    for r in range(per_bank):
                         nc.tensor.transpose(
                             out=back[:, j, r * P : (r + 1) * P],
-                            in_=by_hidden[:, piece * PER_BANK + r, j, :],
-                            identity=ident[:],
+                            in_=by_hidden[:, piece * per_bank + r, j, :],
+                            identity=identity[:],
                         )
-                w_cols = slice(piece * PER_BANK * P, (piece + 1) * PER_BANK * P)
-                nc.scalar.copy(out=grouped[:, w_cols, :], in_=back[:].rearrange("p j w -> p w j"))
+                w_cols = slice(piece * WORD * P, (piece + 1) * WORD * P)
+                nc.scalar.copy(out=grouped[:, w_cols, :], in_=back[:].bitcast(BF16).rearrange("p j w -> p w j"))
             cols = slice(half * H, (half + 1) * H)
             nc.vector.quantize_mx(
                 out=hc_codes[:, k, cols].bitcast(E4M3X4),
@@ -116,10 +123,12 @@ def tile_treelstmcellv2_v_kernel(
                 in_=grouped[:].rearrange("p w j -> p (w j)"),
             )
 
+        for lo in range(0, H, UNIT):
+            load_gate_inputs(0, lo)
+
         for k in range(PASSES):
-            load_gate_inputs(k)
             sum_t = [psum.tile([P, PASS_NODES], F32, name="sum_t%d" % q, tag="bank", bufs=BANKS - 1) for q in range(H_BLOCKS)]
-            pair_max_t = pipe.tile([P, H_BLOCKS, PAIRS * PACK, P], BF16, bufs=1)
+            pair_max_t = pipe.tile([P, W_BLOCKS, PAIRS * PACK, P], F32, bufs=1)
             for g in range(LOADS):
                 pairs = stream.tile([P, PAIR_TILES, SIDE, H], BF16)
                 nc.sync.dma_start(out=pairs[:], in_=pair_v[k * LOADS + g])
@@ -136,50 +145,60 @@ def tile_treelstmcellv2_v_kernel(
                                 start=(b == 0),
                                 stop=(b == SIDE - 1),
                             )
-                for piece in range(H_BLOCKS // PER_BANK):
-                    turned = psum.tile([P, PER_BANK, PAIR_TILES, P], BF16, tag="bank", bufs=BANKS - 1)
-                    for r in range(PER_BANK):
-                        q = piece * PER_BANK + r
-                        for t in range(PAIR_TILES):
-                            nc.tensor.transpose(out=turned[:, r, t, :], in_=pair_max[:, t, q * P : (q + 1) * P], identity=sort[:])
-                        p_cols = slice(g * PAIR_TILES * OCTET, (g + 1) * PAIR_TILES * OCTET)
-                        nc.scalar.copy(
-                            out=pair_max_t[:, q, :, p_cols].rearrange("h e (t r) -> h e t r", r=OCTET),
-                            in_=turned[:, r].rearrange("h t (e r) -> h e t r", r=OCTET),
-                        )
+                pair_max_words = pair_max[:].bitcast(F32)
+                p_cols = slice(g * PAIR_TILES * OCTET, (g + 1) * PAIR_TILES * OCTET)
+                for q in range(W_BLOCKS):
+                    turned = psum.tile([P, PAIR_TILES, P], F32, tag="bank", bufs=BANKS - 1)
+                    for t in range(PAIR_TILES):
+                        nc.tensor.transpose(out=turned[:, t, :], in_=pair_max_words[:, t, q * P : (q + 1) * P], identity=sort[:])
+                    nc.scalar.copy(
+                        out=pair_max_t[:, q, :, p_cols].rearrange("h e (t r) -> h e t r", r=OCTET),
+                        in_=turned[:].rearrange("h t (e r) -> h e t r", r=OCTET),
+                    )
             sum_by_hidden = pipe.tile([P, H_BLOCKS, PACK, P], BF16, tag="by_hidden")
             for q in range(H_BLOCKS):
                 nc.scalar.copy(out=sum_by_hidden[:, q], in_=sum_t[q][:].rearrange("h (p j) -> h j p", j=PACK))
-            quantise_hc(k, 0, sum_by_hidden)
+            quantise_hc(k, 0, sum_by_hidden, ident)
             e_half = PAIRS * PACK // 2
-            two_max_t = pipe.tile([P, H_BLOCKS, e_half, P], BF16, bufs=1)
-            nc.vector.tensor_tensor(out=two_max_t[:], in0=pair_max_t[:, :, 0:e_half, :], in1=pair_max_t[:, :, e_half:, :], op=MAX)
-            max_by_hidden = pipe.tile([P, H_BLOCKS, PACK, P], BF16, tag="by_hidden")
+            four = pair_max_t[:].bitcast(BF16)
+            two_max_t = pipe.tile([P, W_BLOCKS, e_half, WORD * P], BF16, bufs=1)
+            nc.vector.tensor_tensor(out=two_max_t[:], in0=four[:, :, 0:e_half, :], in1=four[:, :, e_half:, :], op=MAX)
+            max_by_hidden = pipe.tile([P, W_BLOCKS, PACK, WORD * P], BF16, tag="by_hidden")
             nc.vector.tensor_tensor(out=max_by_hidden[:], in0=two_max_t[:, :, 0:PACK, :], in1=two_max_t[:, :, PACK:, :], op=MAX)
-            quantise_hc(k, 1, max_by_hidden)
+            quantise_hc(k, 1, max_by_hidden[:].bitcast(F32), ident_f32)
 
-        def column_blocks(rows, lo):
-            return [rows[:, :, lo + w * P : lo + (w + 1) * P] for w in range(TWINS)]
-
-        def blocks(t):
-            return [t[:, w] for w in range(TWINS)]
-
-        def by_column(views):
-            return [v.rearrange("p j c -> p c j") for v in views]
+        for lo in range(0, H, UNIT):
+            load_gate_inputs(1, lo)
 
         def product(dst, in0, scalar, in1, op0, op1):
             for w in range(TWINS):
-                nc.vector.scalar_tensor_tensor(out=dst[:, w], in0=in0[w], scalar=scalar, in1=in1[w], op0=op0, op1=op1)
+                c = slice(w * P, (w + 1) * P)
+                nc.vector.scalar_tensor_tensor(
+                    out=dst[:, :, c], in0=in0[:, :, c], scalar=scalar, in1=in1[:, :, c], op0=op0, op1=op1
+                )
+
+        def grouped_product(dst, in0, scalar, in1, op0, op1):
+            for w in range(TWINS):
+                c = slice(w * P, (w + 1) * P)
+                nc.vector.scalar_tensor_tensor(
+                    out=dst[:, c, :],
+                    in0=in0[:, :, c].rearrange("p j c -> p c j"),
+                    scalar=scalar,
+                    in1=in1[:, :, c].rearrange("p j c -> p c j"),
+                    op0=op0,
+                    op1=op1,
+                )
 
         def quantise_gate(k, gate, lo, grouped):
             nc.vector.quantize_mx(
-                out=d_codes[:, k, gate, lo : lo + TWINS * P].bitcast(E5M2X4),
-                scales=d_scales[:, k, gate, lo : lo + TWINS * P],
-                in_=grouped[:].rearrange("p w c j -> p (w c j)"),
+                out=d_codes[:, k, gate, lo : lo + UNIT].bitcast(E5M2X4),
+                scales=d_scales[:, k, gate, lo : lo + UNIT],
+                in_=grouped[:].rearrange("p c j -> p (c j)"),
             )
 
         def multiply_and_store(gate, lo):
-            for m in range(lo, lo + TWINS * P, P):
+            vector_helps = lo + UNIT == H
+            for m in range(lo, lo + UNIT, P):
                 result = pipe.tile([P, 2 * H], F32, bufs=3)
                 for n in range(2 * H // BANK):
                     n_cols = slice(n * BANK, (n + 1) * BANK)
@@ -194,51 +213,54 @@ def tile_treelstmcellv2_v_kernel(
                             start=(k == 0),
                             stop=(k == PASSES - 1),
                         )
-                    nc.scalar.copy(out=result[:, n_cols], in_=acc[:])
+                    if vector_helps and n % 2 == 1:
+                        nc.vector.tensor_copy(out=result[:, n_cols], in_=acc[:])
+                    else:
+                        nc.scalar.copy(out=result[:, n_cols], in_=acc[:])
                 nc.sync.dma_start(out=out[gate * H + m : gate * H + m + P, :], in_=result[:])
 
-        block = [P, TWINS, PACK, P]
-        grouped_block = [P, TWINS, P, PACK]
+        block = [P, PACK, UNIT]
+        grouped_block = [P, UNIT, PACK]
         for k in range(PASSES):
             last = k == PASSES - 1
-            for lo in range(0, H, TWINS * P):
-                tanh_i = column_blocks(t_i[k], lo)
-                tanh_o = column_blocks(t_o[k], lo)
-                tanh_u = column_blocks(t_u[k], lo)
-                tanh_c = column_blocks(t_c[k], lo)
-                g_h = column_blocks(grad[k], lo)
-                g_c = column_blocks(grad[k], H + lo)
+            for lo in range(0, H, UNIT):
+                cols = slice(lo, lo + UNIT)
+                tanh_i = t_i[k][:, :, cols]
+                tanh_o = t_o[k][:, :, cols]
+                tanh_u = t_u[k][:, :, cols]
+                tanh_c = t_c[k][:, :, cols]
+                g_h = grad[k][:, :, cols]
+                g_c = grad[k][:, :, H + lo : H + lo + UNIT]
                 sq_c = pipe.tile(block, F32)
                 sq_u = pipe.tile(block, F32)
-                for w in range(TWINS):
-                    nc.scalar.activation(out=sq_c[:, w], in_=tanh_c[w], func=SQUARE, scale=0.5)
-                for w in range(TWINS):
-                    nc.scalar.activation(out=sq_u[:, w], in_=tanh_u[w], func=SQUARE)
+                with tc.high_priority():
+                    nc.scalar.activation(out=sq_c[:], in_=tanh_c, func=SQUARE, scale=0.5)
+                    nc.scalar.activation(out=sq_u[:], in_=tanh_u, func=SQUARE)
 
                 gh_so = temp.tile(block, F32, tag="temp")
                 product(gh_so, tanh_o, -1.0, g_h, ADD, MULT)
                 gh_dso = temp.tile(block, F32, tag="temp")
-                product(gh_dso, tanh_o, 1.0, blocks(gh_so), ADD, MULT)
+                product(gh_dso, tanh_o, 1.0, gh_so, ADD, MULT)
                 through_h = temp.tile(block, F32, tag="temp")
-                product(through_h, blocks(sq_c), -0.25, blocks(gh_so), ADD, MULT)
+                product(through_h, sq_c, -0.25, gh_so, ADD, MULT)
                 d_o = pipe.tile(grouped_block, BF16, align_bytes=64)
-                product(d_o, by_column(blocks(gh_dso)), -0.25, by_column(tanh_c), MULT, MULT)
+                grouped_product(d_o, gh_dso, -0.25, tanh_c, MULT, MULT)
                 half_dc = temp.tile(block, F32, tag="temp")
-                product(half_dc, g_c, 0.5, blocks(through_h), MULT, ADD)
+                product(half_dc, g_c, 0.5, through_h, MULT, ADD)
                 quantise_gate(k, 1, lo, d_o)
                 if last:
                     multiply_and_store(1, lo)
                 dc_si = temp.tile(block, F32, tag="temp")
-                product(dc_si, tanh_i, -1.0, blocks(half_dc), ADD, MULT)
-                dc_dsi = temp.tile(block, F32, tag="temp")
-                product(dc_dsi, tanh_i, 1.0, blocks(dc_si), ADD, MULT)
+                product(dc_si, tanh_i, -1.0, half_dc, ADD, MULT)
                 d_u = pipe.tile(grouped_block, BF16, align_bytes=64)
-                product(d_u, by_column(blocks(sq_u)), -1.0, by_column(blocks(dc_si)), ADD, MULT)
-                d_i = pipe.tile(grouped_block, BF16, align_bytes=64)
-                product(d_i, by_column(blocks(dc_dsi)), -0.5, by_column(tanh_u), MULT, MULT)
+                grouped_product(d_u, sq_u, -1.0, dc_si, ADD, MULT)
+                dc_dsi = temp.tile(block, F32, tag="temp")
+                product(dc_dsi, tanh_i, 1.0, dc_si, ADD, MULT)
                 quantise_gate(k, 2, lo, d_u)
                 if last:
                     multiply_and_store(2, lo)
+                d_i = pipe.tile(grouped_block, BF16, align_bytes=64)
+                grouped_product(d_i, dc_dsi, -0.5, tanh_u, MULT, MULT)
                 quantise_gate(k, 0, lo, d_i)
                 if last:
                     multiply_and_store(0, lo)

@@ -34,6 +34,7 @@ OCTET = PAIR_NODES // PACK
 WORD = 2
 W_BLOCKS = H // (WORD * P)
 TWINS = 2
+RESULT_BUFS = 8
 UNIT = TWINS * P
 
 FLOPS = 2 * 3 * H * 2 * H * NODES
@@ -123,8 +124,8 @@ def tile_treelstmcellv2_v_kernel(
                 in_=grouped[:].rearrange("p w j -> p (w j)"),
             )
 
-        for lo in range(0, H, UNIT):
-            load_gate_inputs(0, lo)
+        for k in range(PASSES):
+            load_gate_inputs(k, 0)
 
         for k in range(PASSES):
             sum_t = [psum.tile([P, PASS_NODES], F32, name="sum_t%d" % q, tag="bank", bufs=BANKS - 1) for q in range(H_BLOCKS)]
@@ -161,14 +162,14 @@ def tile_treelstmcellv2_v_kernel(
             quantise_hc(k, 0, sum_by_hidden, ident)
             e_half = PAIRS * PACK // 2
             four = pair_max_t[:].bitcast(BF16)
-            two_max_t = pipe.tile([P, W_BLOCKS, e_half, WORD * P], BF16, bufs=1)
-            nc.vector.tensor_tensor(out=two_max_t[:], in0=four[:, :, 0:e_half, :], in1=four[:, :, e_half:, :], op=MAX)
+            nc.vector.tensor_tensor(out=four[:, :, 0:e_half, :], in0=four[:, :, 0:e_half, :], in1=four[:, :, e_half:, :], op=MAX)
             max_by_hidden = pipe.tile([P, W_BLOCKS, PACK, WORD * P], BF16, tag="by_hidden")
-            nc.vector.tensor_tensor(out=max_by_hidden[:], in0=two_max_t[:, :, 0:PACK, :], in1=two_max_t[:, :, PACK:, :], op=MAX)
+            nc.vector.tensor_tensor(out=max_by_hidden[:], in0=four[:, :, 0:PACK, :], in1=four[:, :, PACK:e_half, :], op=MAX)
             quantise_hc(k, 1, max_by_hidden[:].bitcast(F32), ident_f32)
 
-        for lo in range(0, H, UNIT):
-            load_gate_inputs(1, lo)
+        for lo in range(UNIT, H, UNIT):
+            for k in range(PASSES):
+                load_gate_inputs(k, lo)
 
         def product(dst, in0, scalar, in1, op0, op1):
             for w in range(TWINS):
@@ -197,9 +198,8 @@ def tile_treelstmcellv2_v_kernel(
             )
 
         def multiply_and_store(gate, lo):
-            vector_helps = lo + UNIT == H
+            vector_helps = gate == 0 and lo + UNIT == H
             for m in range(lo, lo + UNIT, P):
-                result = pipe.tile([P, 2 * H], F32, bufs=3)
                 for n in range(2 * H // BANK):
                     n_cols = slice(n * BANK, (n + 1) * BANK)
                     acc = psum.tile([P, BANK], F32, tag="bank", bufs=BANKS - 1)
@@ -213,17 +213,18 @@ def tile_treelstmcellv2_v_kernel(
                             start=(k == 0),
                             stop=(k == PASSES - 1),
                         )
+                    result = pipe.tile([P, BANK], F32, bufs=RESULT_BUFS)
                     if vector_helps and n % 2 == 1:
-                        nc.vector.tensor_copy(out=result[:, n_cols], in_=acc[:])
+                        nc.vector.tensor_copy(out=result[:], in_=acc[:])
                     else:
-                        nc.scalar.copy(out=result[:, n_cols], in_=acc[:])
-                nc.sync.dma_start(out=out[gate * H + m : gate * H + m + P, :], in_=result[:])
+                        nc.scalar.copy(out=result[:], in_=acc[:])
+                    nc.sync.dma_start(out=out[gate * H + m : gate * H + m + P, n_cols], in_=result[:])
 
         block = [P, PACK, UNIT]
         grouped_block = [P, UNIT, PACK]
-        for k in range(PASSES):
-            last = k == PASSES - 1
-            for lo in range(0, H, UNIT):
+        for lo in range(0, H, UNIT):
+            for k in range(PASSES):
+                last = k == PASSES - 1
                 cols = slice(lo, lo + UNIT)
                 tanh_i = t_i[k][:, :, cols]
                 tanh_o = t_o[k][:, :, cols]
@@ -241,10 +242,10 @@ def tile_treelstmcellv2_v_kernel(
                 product(gh_so, tanh_o, -1.0, g_h, ADD, MULT)
                 gh_dso = temp.tile(block, F32, tag="temp")
                 product(gh_dso, tanh_o, 1.0, gh_so, ADD, MULT)
-                through_h = temp.tile(block, F32, tag="temp")
-                product(through_h, sq_c, -0.25, gh_so, ADD, MULT)
                 d_o = pipe.tile(grouped_block, BF16, align_bytes=64)
                 grouped_product(d_o, gh_dso, -0.25, tanh_c, MULT, MULT)
+                through_h = temp.tile(block, F32, tag="temp")
+                product(through_h, sq_c, -0.25, gh_so, ADD, MULT)
                 half_dc = temp.tile(block, F32, tag="temp")
                 product(half_dc, g_c, 0.5, through_h, MULT, ADD)
                 quantise_gate(k, 1, lo, d_o)

@@ -33,9 +33,8 @@ LOADS = PASS_NODES // (PAIR_TILES * PAIR_NODES)
 OCTET = PAIR_NODES // PACK
 WORD = 2
 W_BLOCKS = H // (WORD * P)
-TWINS = 2
 RESULT_BUFS = 8
-UNIT = TWINS * P
+UNIT = 2 * P
 
 FLOPS = 2 * 3 * H * 2 * H * NODES
 BYTES = 2 * NODES * CHILDREN * H + 4 * NODES * 3 * H + 4 * NODES * H + 2 * NODES * 2 * H + 4 * 3 * H * 2 * H
@@ -54,7 +53,6 @@ def tile_treelstmcellv2_v_kernel(
         keep = ctx.enter_context(tc.tile_pool(name="keep", bufs=1))
         stream = ctx.enter_context(tc.tile_pool(name="stream", bufs=3))
         pipe = ctx.enter_context(tc.tile_pool(name="pipe", bufs=2))
-        temp = ctx.enter_context(tc.tile_pool(name="temp", bufs=3))
         psum = ctx.enter_context(tc.psum_pool(name="psum", bufs=1))
 
         ident = keep.tile([P, P], BF16)
@@ -90,18 +88,27 @@ def tile_treelstmcellv2_v_kernel(
             t_c.append(keep.tile([P, PACK, H], F32, name="t_c%d" % k))
             grad.append(keep.tile([P, PACK, 2 * H], BF16, name="grad%d" % k))
 
-        def load_gate_inputs(k, lo):
+        def load_gate_inputs(lo):
             cols = slice(lo, lo + UNIT)
-            nc.sync.dma_start(out=t_o[k][:, :, cols], in_=iou_v[k][:, :, H + lo : H + lo + UNIT])
-            nc.sync.dma_start(out=grad[k][:, :, cols], in_=grad_v[k][:, :, cols])
-            nc.sync.dma_start(out=t_c[k][:, :, cols], in_=cell_v[k][:, :, cols])
-            nc.sync.dma_start(out=grad[k][:, :, H + lo : H + lo + UNIT], in_=grad_v[k][:, :, H + lo : H + lo + UNIT])
-            nc.sync.dma_start(out=t_i[k][:, :, cols], in_=iou_v[k][:, :, cols])
-            nc.sync.dma_start(out=t_u[k][:, :, cols], in_=iou_v[k][:, :, 2 * H + lo : 2 * H + lo + UNIT])
-            nc.scalar.activation(out=t_o[k][:, :, cols], in_=t_o[k][:, :, cols], func=TANH, scale=-0.5)
-            nc.scalar.activation(out=t_c[k][:, :, cols], in_=t_c[k][:, :, cols], func=TANH)
-            nc.scalar.activation(out=t_i[k][:, :, cols], in_=t_i[k][:, :, cols], func=TANH, scale=-0.5)
-            nc.scalar.activation(out=t_u[k][:, :, cols], in_=t_u[k][:, :, cols], func=TANH)
+            for k in range(PASSES):
+                nc.sync.dma_start(out=t_o[k][:, :, cols], in_=iou_v[k][:, :, H + lo : H + lo + UNIT])
+                nc.sync.dma_start(out=grad[k][:, :, cols], in_=grad_v[k][:, :, cols])
+            for k in range(PASSES):
+                nc.sync.dma_start(out=t_c[k][:, :, cols], in_=cell_v[k][:, :, cols])
+            for k in range(PASSES):
+                nc.sync.dma_start(out=grad[k][:, :, H + lo : H + lo + UNIT], in_=grad_v[k][:, :, H + lo : H + lo + UNIT])
+            for k in range(PASSES):
+                nc.sync.dma_start(out=t_i[k][:, :, cols], in_=iou_v[k][:, :, cols])
+            for k in range(PASSES):
+                nc.sync.dma_start(out=t_u[k][:, :, cols], in_=iou_v[k][:, :, 2 * H + lo : 2 * H + lo + UNIT])
+            for k in range(PASSES):
+                nc.scalar.activation(out=t_o[k][:, :, cols], in_=t_o[k][:, :, cols], func=TANH, scale=-0.5)
+            for k in range(PASSES):
+                nc.scalar.activation(out=t_c[k][:, :, cols], in_=t_c[k][:, :, cols], func=TANH)
+            for k in range(PASSES):
+                nc.scalar.activation(out=t_i[k][:, :, cols], in_=t_i[k][:, :, cols], func=TANH, scale=-0.5)
+            for k in range(PASSES):
+                nc.scalar.activation(out=t_u[k][:, :, cols], in_=t_u[k][:, :, cols], func=TANH)
 
         def quantise_hc(k, half, by_hidden, identity):
             grouped = pipe.tile([P, H, PACK], BF16, align_bytes=64)
@@ -124,8 +131,7 @@ def tile_treelstmcellv2_v_kernel(
                 in_=grouped[:].rearrange("p w j -> p (w j)"),
             )
 
-        for k in range(PASSES):
-            load_gate_inputs(k, 0)
+        load_gate_inputs(0)
 
         for k in range(PASSES):
             sum_t = [psum.tile([P, PASS_NODES], F32, name="sum_t%d" % q, tag="bank", bufs=BANKS - 1) for q in range(H_BLOCKS)]
@@ -168,27 +174,20 @@ def tile_treelstmcellv2_v_kernel(
             quantise_hc(k, 1, max_by_hidden[:].bitcast(F32), ident_f32)
 
         for lo in range(UNIT, H, UNIT):
-            for k in range(PASSES):
-                load_gate_inputs(k, lo)
+            load_gate_inputs(lo)
 
         def product(dst, in0, scalar, in1, op0, op1):
-            for w in range(TWINS):
-                c = slice(w * P, (w + 1) * P)
-                nc.vector.scalar_tensor_tensor(
-                    out=dst[:, :, c], in0=in0[:, :, c], scalar=scalar, in1=in1[:, :, c], op0=op0, op1=op1
-                )
+            nc.vector.scalar_tensor_tensor(out=dst, in0=in0, scalar=scalar, in1=in1, op0=op0, op1=op1)
 
         def grouped_product(dst, in0, scalar, in1, op0, op1):
-            for w in range(TWINS):
-                c = slice(w * P, (w + 1) * P)
-                nc.vector.scalar_tensor_tensor(
-                    out=dst[:, c, :],
-                    in0=in0[:, :, c].rearrange("p j c -> p c j"),
-                    scalar=scalar,
-                    in1=in1[:, :, c].rearrange("p j c -> p c j"),
-                    op0=op0,
-                    op1=op1,
-                )
+            nc.vector.scalar_tensor_tensor(
+                out=dst[:],
+                in0=in0.rearrange("p j c -> p c j"),
+                scalar=scalar,
+                in1=in1.rearrange("p j c -> p c j"),
+                op0=op0,
+                op1=op1,
+            )
 
         def quantise_gate(k, gate, lo, grouped):
             nc.vector.quantize_mx(
@@ -222,46 +221,51 @@ def tile_treelstmcellv2_v_kernel(
 
         block = [P, PACK, UNIT]
         grouped_block = [P, UNIT, PACK]
+        both = range(PASSES)
         for lo in range(0, H, UNIT):
-            for k in range(PASSES):
-                last = k == PASSES - 1
-                cols = slice(lo, lo + UNIT)
-                tanh_i = t_i[k][:, :, cols]
-                tanh_o = t_o[k][:, :, cols]
-                tanh_u = t_u[k][:, :, cols]
-                tanh_c = t_c[k][:, :, cols]
-                g_h = grad[k][:, :, cols]
-                g_c = grad[k][:, :, H + lo : H + lo + UNIT]
-                sq_c = pipe.tile(block, F32)
-                sq_u = pipe.tile(block, F32)
-                with tc.high_priority():
-                    nc.scalar.activation(out=sq_c[:], in_=tanh_c, func=SQUARE, scale=0.5)
-                    nc.scalar.activation(out=sq_u[:], in_=tanh_u, func=SQUARE)
+            cols = slice(lo, lo + UNIT)
+            tanh_i = [t_i[k][:, :, cols] for k in both]
+            tanh_o = [t_o[k][:, :, cols] for k in both]
+            tanh_u = [t_u[k][:, :, cols] for k in both]
+            tanh_c = [t_c[k][:, :, cols] for k in both]
+            g_h = [grad[k][:, :, cols] for k in both]
+            g_c = [grad[k][:, :, H + lo : H + lo + UNIT] for k in both]
+            sq_c = [pipe.tile(block, F32, name="sq_c%d" % k, bufs=1) for k in both]
+            sq_u = [pipe.tile(block, F32, name="sq_u%d" % k, bufs=1) for k in both]
+            gh_so = [pipe.tile(block, F32, name="gh_so%d" % k, bufs=1) for k in both]
+            d_o = [pipe.tile(grouped_block, BF16, name="d_o%d" % k, bufs=1, align_bytes=64) for k in both]
+            d_u = [pipe.tile(grouped_block, BF16, name="d_u%d" % k, bufs=1, align_bytes=64) for k in both]
+            d_i = [pipe.tile(grouped_block, BF16, name="d_i%d" % k, bufs=1, align_bytes=64) for k in both]
+            with tc.high_priority():
+                for k in both:
+                    nc.scalar.activation(out=sq_c[k][:], in_=tanh_c[k], func=SQUARE, scale=0.5)
+                for k in both:
+                    nc.scalar.activation(out=sq_u[k][:], in_=tanh_u[k], func=SQUARE)
 
-                gh_so = temp.tile(block, F32, tag="temp")
-                product(gh_so, tanh_o, -1.0, g_h, ADD, MULT)
-                gh_dso = temp.tile(block, F32, tag="temp")
-                product(gh_dso, tanh_o, 1.0, gh_so, ADD, MULT)
-                d_o = pipe.tile(grouped_block, BF16, align_bytes=64)
-                grouped_product(d_o, gh_dso, -0.25, tanh_c, MULT, MULT)
-                through_h = temp.tile(block, F32, tag="temp")
-                product(through_h, sq_c, -0.25, gh_so, ADD, MULT)
-                half_dc = temp.tile(block, F32, tag="temp")
-                product(half_dc, g_c, 0.5, through_h, MULT, ADD)
-                quantise_gate(k, 1, lo, d_o)
-                if last:
-                    multiply_and_store(1, lo)
-                dc_si = temp.tile(block, F32, tag="temp")
-                product(dc_si, tanh_i, -1.0, half_dc, ADD, MULT)
-                d_u = pipe.tile(grouped_block, BF16, align_bytes=64)
-                grouped_product(d_u, sq_u, -1.0, dc_si, ADD, MULT)
-                dc_dsi = temp.tile(block, F32, tag="temp")
-                product(dc_dsi, tanh_i, 1.0, dc_si, ADD, MULT)
-                quantise_gate(k, 2, lo, d_u)
-                if last:
-                    multiply_and_store(2, lo)
-                d_i = pipe.tile(grouped_block, BF16, align_bytes=64)
-                grouped_product(d_i, dc_dsi, -0.5, tanh_u, MULT, MULT)
-                quantise_gate(k, 0, lo, d_i)
-                if last:
-                    multiply_and_store(0, lo)
+            for k in both:
+                product(gh_so[k][:], tanh_o[k], -1.0, g_h[k], ADD, MULT)
+            for k in both:
+                product(tanh_o[k], tanh_o[k], 1.0, gh_so[k][:], ADD, MULT)
+            for k in both:
+                grouped_product(d_o[k], tanh_o[k], -0.25, tanh_c[k], MULT, MULT)
+            for k in both:
+                product(sq_c[k][:], sq_c[k][:], -0.25, gh_so[k][:], ADD, MULT)
+            for k in both:
+                quantise_gate(k, 1, lo, d_o[k])
+            multiply_and_store(1, lo)
+            for k in both:
+                product(sq_c[k][:], g_c[k], 0.5, sq_c[k][:], MULT, ADD)
+            for k in both:
+                product(sq_c[k][:], tanh_i[k], -1.0, sq_c[k][:], ADD, MULT)
+            for k in both:
+                grouped_product(d_u[k], sq_u[k][:], -1.0, sq_c[k][:], ADD, MULT)
+            for k in both:
+                product(tanh_i[k], tanh_i[k], 1.0, sq_c[k][:], ADD, MULT)
+            for k in both:
+                quantise_gate(k, 2, lo, d_u[k])
+            multiply_and_store(2, lo)
+            for k in both:
+                grouped_product(d_i[k], tanh_i[k], -0.5, tanh_u[k], MULT, MULT)
+            for k in both:
+                quantise_gate(k, 0, lo, d_i[k])
+            multiply_and_store(0, lo)

@@ -33,6 +33,7 @@ LOADS = PASS_NODES // (PAIR_TILES * PAIR_NODES)
 OCTET = PAIR_NODES // PACK
 WORD = 2
 W_BLOCKS = H // (WORD * P)
+E_HALF = PAIRS * PACK // 2
 RESULT_BUFS = 8
 UNIT = 2 * P
 
@@ -131,11 +132,36 @@ def tile_treelstmcellv2_v_kernel(
                 in_=grouped[:].rearrange("p w j -> p (w j)"),
             )
 
+        def quantise_sum(k, node_words):
+            grouped = pipe.tile([P, H, PACK], BF16, align_bytes=64)
+            grouped_words = grouped[:].rearrange("p w j -> p (w j)").bitcast(F32)
+            per_bank = H_BLOCKS // W_BLOCKS
+            halves = PACK // WORD
+            for piece in range(W_BLOCKS):
+                back = psum.tile([P, halves, per_bank * P], F32, tag="back")
+                for u in range(halves):
+                    for r in range(per_bank):
+                        nc.tensor.transpose(
+                            out=back[:, u, r * P : (r + 1) * P],
+                            in_=node_words[:, piece * per_bank + r, u, :],
+                            identity=ident_f32[:],
+                        )
+                width = halves * per_bank * P
+                nc.scalar.copy(
+                    out=grouped_words[:, piece * width : (piece + 1) * width].rearrange("p (w u) -> p w u", u=halves),
+                    in_=back[:].rearrange("p u w -> p w u"),
+                )
+            nc.vector.quantize_mx(
+                out=hc_codes[:, k, 0:H].bitcast(E4M3X4),
+                scales=hc_scales[:, k, 0:H],
+                in_=grouped[:].rearrange("p w j -> p (w j)"),
+            )
+
         load_gate_inputs(0)
 
         for k in range(PASSES):
             sum_t = [psum.tile([P, PASS_NODES], F32, name="sum_t%d" % q, tag="bank", bufs=BANKS - 1) for q in range(H_BLOCKS)]
-            pair_max_t = pipe.tile([P, W_BLOCKS, PAIRS * PACK, P], F32, bufs=1)
+            two_max_t = pipe.tile([P, W_BLOCKS, E_HALF, P], F32, bufs=1)
             for g in range(LOADS):
                 pairs = stream.tile([P, PAIR_TILES, SIDE, H], BF16)
                 nc.sync.dma_start(out=pairs[:], in_=pair_v[k * LOADS + g])
@@ -159,18 +185,26 @@ def tile_treelstmcellv2_v_kernel(
                     for t in range(PAIR_TILES):
                         nc.tensor.transpose(out=turned[:, t, :], in_=pair_max_words[:, t, q * P : (q + 1) * P], identity=sort[:])
                     nc.scalar.copy(
-                        out=pair_max_t[:, q, :, p_cols].rearrange("h e (t r) -> h e t r", r=OCTET),
-                        in_=turned[:].rearrange("h t (e r) -> h e t r", r=OCTET),
+                        out=two_max_t[:, q, :, p_cols].rearrange("h e (t r) -> h e t r", r=OCTET),
+                        in_=turned[:, :, P // 2 :].rearrange("h t (e r) -> h e t r", r=OCTET),
                     )
-            sum_by_hidden = pipe.tile([P, H_BLOCKS, PACK, P], BF16, tag="by_hidden")
+                    upper = two_max_t[:, q, :, p_cols].bitcast(BF16).rearrange("h e (t x) -> h e t x", x=WORD * OCTET)
+                    nc.vector.tensor_tensor(
+                        out=upper,
+                        in0=turned[:, :, 0 : P // 2].bitcast(BF16).rearrange("h t (e x) -> h e t x", x=WORD * OCTET),
+                        in1=upper,
+                        op=MAX,
+                    )
+            sum_by_hidden = pipe.tile([P, H_BLOCKS, PACK // WORD, WORD * P], BF16, tag="by_hidden")
             for q in range(H_BLOCKS):
-                nc.scalar.copy(out=sum_by_hidden[:, q], in_=sum_t[q][:].rearrange("h (p j) -> h j p", j=PACK))
-            quantise_hc(k, 0, sum_by_hidden, ident)
-            e_half = PAIRS * PACK // 2
-            four = pair_max_t[:].bitcast(BF16)
-            nc.vector.tensor_tensor(out=four[:, :, 0:e_half, :], in0=four[:, :, 0:e_half, :], in1=four[:, :, e_half:, :], op=MAX)
+                nc.scalar.copy(
+                    out=sum_by_hidden[:, q].rearrange("h u (p e) -> h u p e", e=WORD),
+                    in_=sum_t[q][:].rearrange("h (p u e) -> h u p e", u=PACK // WORD, e=WORD),
+                )
+            quantise_sum(k, sum_by_hidden[:].bitcast(F32))
+            two = two_max_t[:].bitcast(BF16)
             max_by_hidden = pipe.tile([P, W_BLOCKS, PACK, WORD * P], BF16, tag="by_hidden")
-            nc.vector.tensor_tensor(out=max_by_hidden[:], in0=four[:, :, 0:PACK, :], in1=four[:, :, PACK:e_half, :], op=MAX)
+            nc.vector.tensor_tensor(out=max_by_hidden[:], in0=two[:, :, 0:PACK, :], in1=two[:, :, PACK:, :], op=MAX)
             quantise_hc(k, 1, max_by_hidden[:].bitcast(F32), ident_f32)
 
         for lo in range(UNIT, H, UNIT):

@@ -52,7 +52,7 @@ def tile_treelstmcellv2_v_kernel(
 
     with ExitStack() as ctx:
         keep = ctx.enter_context(tc.tile_pool(name="keep", bufs=1))
-        stream = ctx.enter_context(tc.tile_pool(name="stream", bufs=3))
+        stream = ctx.enter_context(tc.tile_pool(name="stream", bufs=4))
         pipe = ctx.enter_context(tc.tile_pool(name="pipe", bufs=2))
         psum = ctx.enter_context(tc.psum_pool(name="psum", bufs=1))
 
@@ -102,43 +102,74 @@ def tile_treelstmcellv2_v_kernel(
                 nc.sync.dma_start(out=t_i[k][:, :, cols], in_=iou_v[k][:, :, cols])
             for k in range(PASSES):
                 nc.sync.dma_start(out=t_u[k][:, :, cols], in_=iou_v[k][:, :, 2 * H + lo : 2 * H + lo + UNIT])
-            for k in range(PASSES):
-                nc.scalar.activation(out=t_o[k][:, :, cols], in_=t_o[k][:, :, cols], func=TANH, scale=-0.5)
-            for k in range(PASSES):
-                nc.scalar.activation(out=t_c[k][:, :, cols], in_=t_c[k][:, :, cols], func=TANH)
-            for k in range(PASSES):
-                nc.scalar.activation(out=t_i[k][:, :, cols], in_=t_i[k][:, :, cols], func=TANH, scale=-0.5)
-            for k in range(PASSES):
-                nc.scalar.activation(out=t_u[k][:, :, cols], in_=t_u[k][:, :, cols], func=TANH)
 
-        def quantise_hc(k, half, by_hidden, identity):
-            grouped = pipe.tile([P, H, PACK], BF16, align_bytes=64)
-            per_bank = by_hidden.shape[1] // W_BLOCKS
-            for piece in range(W_BLOCKS):
-                back = psum.tile([P, PACK, per_bank * P], by_hidden.dtype, tag="back")
-                for j in range(PACK):
-                    for r in range(per_bank):
-                        nc.tensor.transpose(
-                            out=back[:, j, r * P : (r + 1) * P],
-                            in_=by_hidden[:, piece * per_bank + r, j, :],
-                            identity=identity[:],
+        both = range(PASSES)
+        ctx.enter_context(tc.manual_schedule(engines={mybir.EngineType.DVE, mybir.EngineType.SP}))
+
+        sum_t = {}
+        two_max_t = {}
+        turned = {}
+        grouped = {}
+
+        def mailbox_load(k, g):
+            if g == 0:
+                sum_t[k] = [
+                    psum.tile([P, PASS_NODES], F32, name="sum_t%d" % q, tag="bank", bufs=BANKS) for q in range(H_BLOCKS)
+                ]
+                two_max_t[k] = pipe.tile([P, W_BLOCKS, E_HALF, P], F32, name="two_max_t")
+            pairs = stream.tile([P, PAIR_TILES, SIDE, H], BF16)
+            nc.sync.dma_start(out=pairs[:], in_=pair_v[k * LOADS + g])
+            pair_max = pipe.tile([P, PAIR_TILES, H], BF16)
+            nc.vector.tensor_tensor(out=pair_max[:], in0=pairs[:, :, 0, :], in1=pairs[:, :, 1, :], op=MAX)
+            for q in range(H_BLOCKS):
+                for t in range(PAIR_TILES):
+                    first = (g * PAIR_TILES + t) * PAIR_NODES
+                    for b in range(SIDE):
+                        nc.tensor.matmul(
+                            out=sum_t[k][q][:, first : first + PAIR_NODES],
+                            lhsT=pairs[:, t, b, q * P : (q + 1) * P],
+                            rhs=pick[:],
+                            start=(b == 0),
+                            stop=(b == SIDE - 1),
                         )
-                w_cols = slice(piece * WORD * P, (piece + 1) * WORD * P)
-                nc.scalar.copy(out=grouped[:, w_cols, :], in_=back[:].bitcast(BF16).rearrange("p j w -> p w j"))
-            cols = slice(half * H, (half + 1) * H)
-            nc.vector.quantize_mx(
-                out=hc_codes[:, k, cols].bitcast(E4M3X4),
-                scales=hc_scales[:, k, cols],
-                in_=grouped[:].rearrange("p w j -> p (w j)"),
-            )
+            pair_max_words = pair_max[:].bitcast(F32)
+            p_cols = slice(g * PAIR_TILES * OCTET, (g + 1) * PAIR_TILES * OCTET)
+            for q in range(W_BLOCKS):
+                turned[(k, g, q)] = psum.tile([P, PAIR_TILES, P], F32, name="turned", tag="bank", bufs=BANKS)
+                for t in range(PAIR_TILES):
+                    nc.tensor.transpose(
+                        out=turned[(k, g, q)][:, t, :], in_=pair_max_words[:, t, q * P : (q + 1) * P], identity=sort[:]
+                    )
+                nc.scalar.copy(
+                    out=two_max_t[k][:, q, :, p_cols].rearrange("h e (t r) -> h e t r", r=OCTET),
+                    in_=turned[(k, g, q)][:, :, P // 2 :].rearrange("h t (e r) -> h e t r", r=OCTET),
+                )
 
-        def quantise_sum(k, node_words):
-            grouped = pipe.tile([P, H, PACK], BF16, align_bytes=64)
-            grouped_words = grouped[:].rearrange("p w j -> p (w j)").bitcast(F32)
+        def two_max(k, g):
+            p_cols = slice(g * PAIR_TILES * OCTET, (g + 1) * PAIR_TILES * OCTET)
+            for q in range(W_BLOCKS):
+                upper = two_max_t[k][:, q, :, p_cols].bitcast(BF16).rearrange("h e (t x) -> h e t x", x=WORD * OCTET)
+                nc.vector.tensor_tensor(
+                    out=upper,
+                    in0=turned[(k, g, q)][:, :, 0 : P // 2].bitcast(BF16).rearrange("h t (e x) -> h e t x", x=WORD * OCTET),
+                    in1=upper,
+                    op=MAX,
+                )
+
+        def sums_back(k):
+            sum_by_hidden = pipe.tile([P, H_BLOCKS, PACK // WORD, WORD * P], BF16, tag="by_hidden")
+            for q in range(H_BLOCKS):
+                nc.scalar.copy(
+                    out=sum_by_hidden[:, q].rearrange("h u (p e) -> h u p e", e=WORD),
+                    in_=sum_t[k][q][:].rearrange("h (p u e) -> h u p e", u=PACK // WORD, e=WORD),
+                )
+            node_words = sum_by_hidden[:].bitcast(F32)
+            grouped[(k, 0)] = pipe.tile([P, H, PACK], BF16, name="grouped", align_bytes=64)
+            grouped_words = grouped[(k, 0)][:].rearrange("p w j -> p (w j)").bitcast(F32)
             per_bank = H_BLOCKS // W_BLOCKS
             halves = PACK // WORD
             for piece in range(W_BLOCKS):
-                back = psum.tile([P, halves, per_bank * P], F32, tag="back")
+                back = psum.tile([P, halves, per_bank * P], F32, name="back", tag="bank", bufs=BANKS)
                 for u in range(halves):
                     for r in range(per_bank):
                         nc.tensor.transpose(
@@ -151,83 +182,26 @@ def tile_treelstmcellv2_v_kernel(
                     out=grouped_words[:, piece * width : (piece + 1) * width].rearrange("p (w u) -> p w u", u=halves),
                     in_=back[:].rearrange("p u w -> p w u"),
                 )
-            nc.vector.quantize_mx(
-                out=hc_codes[:, k, 0:H].bitcast(E4M3X4),
-                scales=hc_scales[:, k, 0:H],
-                in_=grouped[:].rearrange("p w j -> p (w j)"),
-            )
 
-        load_gate_inputs(0)
-
-        for k in range(PASSES):
-            sum_t = [psum.tile([P, PASS_NODES], F32, name="sum_t%d" % q, tag="bank", bufs=BANKS - 1) for q in range(H_BLOCKS)]
-            two_max_t = pipe.tile([P, W_BLOCKS, E_HALF, P], F32, bufs=1)
-            for g in range(LOADS):
-                pairs = stream.tile([P, PAIR_TILES, SIDE, H], BF16)
-                nc.sync.dma_start(out=pairs[:], in_=pair_v[k * LOADS + g])
-                pair_max = pipe.tile([P, PAIR_TILES, H], BF16)
-                nc.vector.tensor_tensor(out=pair_max[:], in0=pairs[:, :, 0, :], in1=pairs[:, :, 1, :], op=MAX)
-                for q in range(H_BLOCKS):
-                    for t in range(PAIR_TILES):
-                        first = (g * PAIR_TILES + t) * PAIR_NODES
-                        for b in range(SIDE):
-                            nc.tensor.matmul(
-                                out=sum_t[q][:, first : first + PAIR_NODES],
-                                lhsT=pairs[:, t, b, q * P : (q + 1) * P],
-                                rhs=pick[:],
-                                start=(b == 0),
-                                stop=(b == SIDE - 1),
-                            )
-                pair_max_words = pair_max[:].bitcast(F32)
-                p_cols = slice(g * PAIR_TILES * OCTET, (g + 1) * PAIR_TILES * OCTET)
-                for q in range(W_BLOCKS):
-                    turned = psum.tile([P, PAIR_TILES, P], F32, tag="bank", bufs=BANKS - 1)
-                    for t in range(PAIR_TILES):
-                        nc.tensor.transpose(out=turned[:, t, :], in_=pair_max_words[:, t, q * P : (q + 1) * P], identity=sort[:])
-                    nc.scalar.copy(
-                        out=two_max_t[:, q, :, p_cols].rearrange("h e (t r) -> h e t r", r=OCTET),
-                        in_=turned[:, :, P // 2 :].rearrange("h t (e r) -> h e t r", r=OCTET),
-                    )
-                    upper = two_max_t[:, q, :, p_cols].bitcast(BF16).rearrange("h e (t x) -> h e t x", x=WORD * OCTET)
-                    nc.vector.tensor_tensor(
-                        out=upper,
-                        in0=turned[:, :, 0 : P // 2].bitcast(BF16).rearrange("h t (e x) -> h e t x", x=WORD * OCTET),
-                        in1=upper,
-                        op=MAX,
-                    )
-            sum_by_hidden = pipe.tile([P, H_BLOCKS, PACK // WORD, WORD * P], BF16, tag="by_hidden")
-            for q in range(H_BLOCKS):
-                nc.scalar.copy(
-                    out=sum_by_hidden[:, q].rearrange("h u (p e) -> h u p e", e=WORD),
-                    in_=sum_t[q][:].rearrange("h (p u e) -> h u p e", u=PACK // WORD, e=WORD),
-                )
-            quantise_sum(k, sum_by_hidden[:].bitcast(F32))
-            two = two_max_t[:].bitcast(BF16)
+        def max_back(k):
+            two = two_max_t[k][:].bitcast(BF16)
             max_by_hidden = pipe.tile([P, W_BLOCKS, PACK, WORD * P], BF16, tag="by_hidden")
             nc.vector.tensor_tensor(out=max_by_hidden[:], in0=two[:, :, 0:PACK, :], in1=two[:, :, PACK:, :], op=MAX)
-            quantise_hc(k, 1, max_by_hidden[:].bitcast(F32), ident_f32)
+            words = max_by_hidden[:].bitcast(F32)
+            grouped[(k, 1)] = pipe.tile([P, H, PACK], BF16, name="grouped", align_bytes=64)
+            for piece in range(W_BLOCKS):
+                back = psum.tile([P, PACK, P], F32, name="back", tag="bank", bufs=BANKS)
+                for j in range(PACK):
+                    nc.tensor.transpose(out=back[:, j, :], in_=words[:, piece, j, :], identity=ident_f32[:])
+                w_cols = slice(piece * WORD * P, (piece + 1) * WORD * P)
+                nc.scalar.copy(out=grouped[(k, 1)][:, w_cols, :], in_=back[:].bitcast(BF16).rearrange("p j w -> p w j"))
 
-        for lo in range(UNIT, H, UNIT):
-            load_gate_inputs(lo)
-
-        def product(dst, in0, scalar, in1, op0, op1):
-            nc.vector.scalar_tensor_tensor(out=dst, in0=in0, scalar=scalar, in1=in1, op0=op0, op1=op1)
-
-        def grouped_product(dst, in0, scalar, in1, op0, op1):
-            nc.vector.scalar_tensor_tensor(
-                out=dst[:],
-                in0=in0.rearrange("p j c -> p c j"),
-                scalar=scalar,
-                in1=in1.rearrange("p j c -> p c j"),
-                op0=op0,
-                op1=op1,
-            )
-
-        def quantise_gate(k, gate, lo, grouped):
+        def quantise_hc(k, half):
+            cols = slice(half * H, (half + 1) * H)
             nc.vector.quantize_mx(
-                out=d_codes[:, k, gate, lo : lo + UNIT].bitcast(E5M2X4),
-                scales=d_scales[:, k, gate, lo : lo + UNIT],
-                in_=grouped[:].rearrange("p c j -> p (c j)"),
+                out=hc_codes[:, k, cols].bitcast(E4M3X4),
+                scales=hc_scales[:, k, cols],
+                in_=grouped[(k, half)][:].rearrange("p w j -> p (w j)"),
             )
 
         def multiply_and_store(gate, lo):
@@ -235,8 +209,8 @@ def tile_treelstmcellv2_v_kernel(
             for m in range(lo, lo + UNIT, P):
                 for n in range(2 * H // BANK):
                     n_cols = slice(n * BANK, (n + 1) * BANK)
-                    acc = psum.tile([P, BANK], F32, tag="bank", bufs=BANKS - 1)
-                    for k in range(PASSES):
+                    acc = psum.tile([P, BANK], F32, tag="bank", bufs=BANKS)
+                    for k in both:
                         nc.tensor.matmul_mx(
                             out=acc[:],
                             lhsT=d_codes[:, k, gate, m : m + P].bitcast(E5M2X4),
@@ -255,8 +229,8 @@ def tile_treelstmcellv2_v_kernel(
 
         block = [P, PACK, UNIT]
         grouped_block = [P, UNIT, PACK]
-        both = range(PASSES)
-        for lo in range(0, H, UNIT):
+
+        def chain(lo):
             cols = slice(lo, lo + UNIT)
             tanh_i = [t_i[k][:, :, cols] for k in both]
             tanh_o = [t_o[k][:, :, cols] for k in both]
@@ -267,39 +241,104 @@ def tile_treelstmcellv2_v_kernel(
             sq_c = [pipe.tile(block, F32, name="sq_c%d" % k, bufs=1) for k in both]
             sq_u = [pipe.tile(block, F32, name="sq_u%d" % k, bufs=1) for k in both]
             gh_so = [pipe.tile(block, F32, name="gh_so%d" % k, bufs=1) for k in both]
-            d_o = [pipe.tile(grouped_block, BF16, name="d_o%d" % k, bufs=1, align_bytes=64) for k in both]
-            d_u = [pipe.tile(grouped_block, BF16, name="d_u%d" % k, bufs=1, align_bytes=64) for k in both]
-            d_i = [pipe.tile(grouped_block, BF16, name="d_i%d" % k, bufs=1, align_bytes=64) for k in both]
-            with tc.high_priority():
-                for k in both:
-                    nc.scalar.activation(out=sq_c[k][:], in_=tanh_c[k], func=SQUARE, scale=0.5)
-                for k in both:
-                    nc.scalar.activation(out=sq_u[k][:], in_=tanh_u[k], func=SQUARE)
+            d = {
+                gate: [pipe.tile(grouped_block, BF16, name="d%d%d" % (gate, k), bufs=1, align_bytes=64) for k in both]
+                for gate in range(3)
+            }
+            def product(dst, in0, scalar, in1, op0, op1):
+                nc.vector.scalar_tensor_tensor(out=dst, in0=in0, scalar=scalar, in1=in1, op0=op0, op1=op1)
 
-            for k in both:
-                product(gh_so[k][:], tanh_o[k], -1.0, g_h[k], ADD, MULT)
-            for k in both:
-                product(tanh_o[k], tanh_o[k], 1.0, gh_so[k][:], ADD, MULT)
-            for k in both:
-                grouped_product(d_o[k], tanh_o[k], -0.25, tanh_c[k], MULT, MULT)
-            for k in both:
-                product(sq_c[k][:], sq_c[k][:], -0.25, gh_so[k][:], ADD, MULT)
-            for k in both:
-                quantise_gate(k, 1, lo, d_o[k])
-            multiply_and_store(1, lo)
-            for k in both:
-                product(sq_c[k][:], g_c[k], 0.5, sq_c[k][:], MULT, ADD)
-            for k in both:
-                product(sq_c[k][:], tanh_i[k], -1.0, sq_c[k][:], ADD, MULT)
-            for k in both:
-                grouped_product(d_u[k], sq_u[k][:], -1.0, sq_c[k][:], ADD, MULT)
-            for k in both:
-                product(tanh_i[k], tanh_i[k], 1.0, sq_c[k][:], ADD, MULT)
-            for k in both:
-                quantise_gate(k, 2, lo, d_u[k])
-            multiply_and_store(2, lo)
-            for k in both:
-                grouped_product(d_i[k], tanh_i[k], -0.5, tanh_u[k], MULT, MULT)
-            for k in both:
-                quantise_gate(k, 0, lo, d_i[k])
-            multiply_and_store(0, lo)
+            def grouped_product(dst, in0, scalar, in1, op0, op1):
+                product(dst[:], in0.rearrange("p j c -> p c j"), scalar, in1.rearrange("p j c -> p c j"), op0, op1)
+
+            def quantise(gate, k):
+                nc.vector.quantize_mx(
+                    out=d_codes[:, k, gate, cols].bitcast(E5M2X4),
+                    scales=d_scales[:, k, gate, cols],
+                    in_=d[gate][k][:].rearrange("p c j -> p (c j)"),
+                )
+
+            def step(name, k):
+                x = sq_c[k][:]
+                if name == "tanh_o":
+                    nc.scalar.activation(out=tanh_o[k], in_=tanh_o[k], func=TANH, scale=-0.5)
+                elif name == "tanh_c":
+                    nc.scalar.activation(out=tanh_c[k], in_=tanh_c[k], func=TANH)
+                elif name == "sq_c":
+                    nc.scalar.activation(out=x, in_=tanh_c[k], func=SQUARE, scale=0.5)
+                elif name == "tanh_i":
+                    nc.scalar.activation(out=tanh_i[k], in_=tanh_i[k], func=TANH, scale=-0.5)
+                elif name == "tanh_u":
+                    nc.scalar.activation(out=tanh_u[k], in_=tanh_u[k], func=TANH)
+                elif name == "sq_u":
+                    nc.scalar.activation(out=sq_u[k][:], in_=tanh_u[k], func=SQUARE)
+                elif name == "gh_so":
+                    product(gh_so[k][:], tanh_o[k], -1.0, g_h[k], ADD, MULT)
+                elif name == "gh_dso":
+                    product(tanh_o[k], tanh_o[k], 1.0, gh_so[k][:], ADD, MULT)
+                elif name == "d_o":
+                    grouped_product(d[1][k], tanh_o[k], -0.25, tanh_c[k], MULT, MULT)
+                elif name == "through_h":
+                    product(x, x, -0.25, gh_so[k][:], ADD, MULT)
+                elif name == "half_dc":
+                    product(x, g_c[k], 0.5, x, MULT, ADD)
+                elif name == "dc_si":
+                    product(x, tanh_i[k], -1.0, x, ADD, MULT)
+                elif name == "d_u":
+                    grouped_product(d[2][k], sq_u[k][:], -1.0, x, ADD, MULT)
+                elif name == "dc_dsi":
+                    product(tanh_i[k], tanh_i[k], 1.0, x, ADD, MULT)
+                elif name == "d_i":
+                    grouped_product(d[0][k], tanh_i[k], -0.5, tanh_u[k], MULT, MULT)
+                elif name == "q_o":
+                    quantise(1, k)
+                elif name == "q_u":
+                    quantise(2, k)
+                else:
+                    quantise(0, k)
+
+            return step
+
+        def steps(step, names):
+            for name in names:
+                for k in both:
+                    step(name, k)
+
+        load_gate_inputs(0)
+        first = chain(0)
+        steps(first, ("tanh_o", "tanh_c", "sq_c", "tanh_i", "tanh_u", "sq_u"))
+        steps(first, ("gh_so", "gh_dso", "d_o", "through_h", "q_o", "half_dc", "dc_si", "d_u"))
+        rest = [(name, k) for name in ("dc_dsi", "q_u", "d_i", "q_i") for k in both]
+        loads = [(k, g) for k in both for g in range(LOADS)]
+        for n in range(len(loads)):
+            mailbox_load(loads[n][0], loads[n][1])
+            first(rest[n][0], rest[n][1])
+            if n > 0:
+                two_max(loads[n - 1][0], loads[n - 1][1])
+            if n == LOADS:
+                max_back(0)
+            if n == LOADS - 1:
+                sums_back(0)
+            if n == LOADS + 1:
+                quantise_hc(0, 0)
+            if n == LOADS + 2:
+                quantise_hc(0, 1)
+        load_gate_inputs(UNIT)
+        second = chain(UNIT)
+        sums_back(PASSES - 1)
+        steps(second, ("tanh_o", "gh_so"))
+        two_max(PASSES - 1, LOADS - 1)
+        max_back(PASSES - 1)
+        steps(second, ("gh_dso", "tanh_c", "sq_c"))
+        quantise_hc(PASSES - 1, 0)
+        steps(second, ("d_o",))
+        quantise_hc(PASSES - 1, 1)
+        steps(second, ("tanh_i", "tanh_u", "sq_u"))
+        for gate in (1, 2, 0):
+            multiply_and_store(gate, 0)
+        steps(second, ("through_h", "q_o"))
+        multiply_and_store(1, UNIT)
+        steps(second, ("half_dc", "dc_si", "d_u", "dc_dsi", "q_u"))
+        multiply_and_store(2, UNIT)
+        steps(second, ("d_i", "q_i"))
+        multiply_and_store(0, UNIT)

@@ -230,7 +230,7 @@ def tile_treelstmcellv2_v_kernel(
         block = [P, PACK, UNIT]
         grouped_block = [P, UNIT, PACK]
 
-        def chain(lo):
+        def chain(lo, by_scalar):
             cols = slice(lo, lo + UNIT)
             tanh_i = [t_i[k][:, :, cols] for k in both]
             tanh_o = [t_o[k][:, :, cols] for k in both]
@@ -248,8 +248,13 @@ def tile_treelstmcellv2_v_kernel(
             def product(dst, in0, scalar, in1, op0, op1):
                 nc.vector.scalar_tensor_tensor(out=dst, in0=in0, scalar=scalar, in1=in1, op0=op0, op1=op1)
 
-            def grouped_product(dst, in0, scalar, in1, op0, op1):
-                product(dst[:], in0.rearrange("p j c -> p c j"), scalar, in1.rearrange("p j c -> p c j"), op0, op1)
+            def grouped_product(gate, k, in0, scalar, in1, op0, op1):
+                if gate in by_scalar:
+                    flat = pipe.tile(block, BF16, name="flat%d%d" % (gate, k), bufs=1)
+                    product(flat[:], in0, scalar, in1, op0, op1)
+                    nc.scalar.copy(out=d[gate][k][:], in_=flat[:].rearrange("p j c -> p c j"))
+                else:
+                    product(d[gate][k][:], in0.rearrange("p j c -> p c j"), scalar, in1.rearrange("p j c -> p c j"), op0, op1)
 
             def quantise(gate, k):
                 nc.vector.quantize_mx(
@@ -277,7 +282,7 @@ def tile_treelstmcellv2_v_kernel(
                 elif name == "gh_dso":
                     product(tanh_o[k], tanh_o[k], 1.0, gh_so[k][:], ADD, MULT)
                 elif name == "d_o":
-                    grouped_product(d[1][k], tanh_o[k], -0.25, tanh_c[k], MULT, MULT)
+                    grouped_product(1, k, tanh_o[k], -0.25, tanh_c[k], MULT, MULT)
                 elif name == "through_h":
                     product(x, x, -0.25, gh_so[k][:], ADD, MULT)
                 elif name == "half_dc":
@@ -285,11 +290,11 @@ def tile_treelstmcellv2_v_kernel(
                 elif name == "dc_si":
                     product(x, tanh_i[k], -1.0, x, ADD, MULT)
                 elif name == "d_u":
-                    grouped_product(d[2][k], sq_u[k][:], -1.0, x, ADD, MULT)
+                    grouped_product(2, k, sq_u[k][:], -1.0, x, ADD, MULT)
                 elif name == "dc_dsi":
                     product(tanh_i[k], tanh_i[k], 1.0, x, ADD, MULT)
                 elif name == "d_i":
-                    grouped_product(d[0][k], tanh_i[k], -0.5, tanh_u[k], MULT, MULT)
+                    grouped_product(0, k, tanh_i[k], -0.5, tanh_u[k], MULT, MULT)
                 elif name == "q_o":
                     quantise(1, k)
                 elif name == "q_u":
@@ -305,9 +310,9 @@ def tile_treelstmcellv2_v_kernel(
                     step(name, k)
 
         load_gate_inputs(0)
-        first = chain(0)
+        first = chain(0, (1, 2))
         steps(first, ("tanh_o", "tanh_c", "sq_c", "tanh_i", "tanh_u", "sq_u"))
-        steps(first, ("gh_so", "gh_dso", "d_o", "through_h", "q_o", "half_dc", "dc_si", "d_u"))
+        steps(first, ("gh_so", "gh_dso", "d_o", "through_h", "half_dc", "dc_si", "d_u", "q_o"))
         rest = [(name, k) for name in ("dc_dsi", "q_u", "d_i", "q_i") for k in both]
         loads = [(k, g) for k in both for g in range(LOADS)]
         for n in range(len(loads)):
@@ -324,7 +329,7 @@ def tile_treelstmcellv2_v_kernel(
             if n == LOADS + 2:
                 quantise_hc(0, 1)
         load_gate_inputs(UNIT)
-        second = chain(UNIT)
+        second = chain(UNIT, ())
         sums_back(PASSES - 1)
         steps(second, ("tanh_o", "gh_so"))
         two_max(PASSES - 1, LOADS - 1)

from contextlib import ExitStack

import concourse.mybir as mybir
from concourse.masks import make_identity

F32 = mybir.dt.float32
BF16 = mybir.dt.bfloat16
U32 = mybir.dt.uint32
U8 = mybir.dt.uint8
E4M3X4 = mybir.dt.float8_e4m3fn_x4
E5M2X4 = mybir.dt.float8_e5m2_x4
ADD = mybir.AluOpType.add
MULT = mybir.AluOpType.mult
MAX = mybir.AluOpType.max
TANH = mybir.ActivationFunctionType.Tanh
SQUARE = mybir.ActivationFunctionType.Square

P = 128
PACK = 4
NODES = 1024
CHILDREN = 8
H = 512
PASSES = NODES // (P * PACK)
PASS_NODES = P * PACK
BANK = 512
BANKS = 8
H_BLOCKS = H // P
SIDE = 2
PAIRS = CHILDREN // SIDE
PAIR_NODES = P // PAIRS
PAIR_TILES = 4
LOADS = PASS_NODES // (PAIR_TILES * PAIR_NODES)
OCTET = PAIR_NODES // PACK
WORD = 2
W_BLOCKS = H // (WORD * P)
E_HALF = PAIRS * PACK // 2
RESULT_BUFS = 8
UNIT = 2 * P

FLOPS = 2 * 3 * H * 2 * H * NODES
BYTES = 2 * NODES * CHILDREN * H + 4 * NODES * 3 * H + 4 * NODES * H + 2 * NODES * 2 * H + 4 * 3 * H * 2 * H


def tile_treelstmcellv2_v_kernel(
    tc, mailbox_h, mailbox_c, U_iou_w, b_iou, U_f_w, U_f_b, iou, c, grad_out, out
):
    nc = tc.nc
    iou_v = iou.rearrange("(k p j) w -> k p j w", p=P, j=PACK)
    cell_v = c.rearrange("(k p j) w -> k p j w", p=P, j=PACK)
    grad_v = grad_out.rearrange("(k p j) w -> k p j w", p=P, j=PACK)
    pair_v = mailbox_h.rearrange("(g t n) (a b) h -> g (n a) t b h", t=PAIR_TILES, n=PAIR_NODES, b=SIDE)

    with ExitStack() as ctx:
        keep = ctx.enter_context(tc.tile_pool(name="keep", bufs=1))
        stream = ctx.enter_context(tc.tile_pool(name="stream", bufs=4))
        pipe = ctx.enter_context(tc.tile_pool(name="pipe", bufs=2))
        psum = ctx.enter_context(tc.psum_pool(name="psum", bufs=1))

        ident = keep.tile([P, P], BF16)
        make_identity(nc, ident[:])
        pick_f32 = keep.tile([P, PAIR_NODES], F32)
        nc.vector.tensor_reduce(
            out=pick_f32[:], in_=ident[:].rearrange("p (n a) -> p n a", a=PAIRS), axis=mybir.AxisListType.X, op=ADD
        )
        pick = keep.tile([P, PAIR_NODES], BF16)
        nc.vector.tensor_copy(out=pick[:], in_=pick_f32[:])
        ident_f32 = keep.tile([P, P], F32)
        make_identity(nc, ident_f32[:])
        sort = keep.tile([P, P], F32)
        nc.vector.tensor_copy(
            out=sort[:].rearrange("p (a j r) -> p a j r", a=PAIRS, j=PACK),
            in_=ident_f32[:].rearrange("p (r j a) -> p a j r", a=PAIRS, j=PACK),
        )

        hc_codes = keep.tile([P, PASSES, 2 * H], U32, align_bytes=64)
        hc_scales = keep.tile([P, PASSES, 2 * H], U8, align_bytes=64)
        d_codes = keep.tile([P, PASSES, 3, H], U32, align_bytes=64)
        d_scales = keep.tile([P, PASSES, 3, H], U8, align_bytes=64)

        t_i = []
        t_o = []
        t_u = []
        t_c = []
        grad = []
        for k in range(PASSES):
            t_i.append(keep.tile([P, PACK, H], F32, name="t_i%d" % k))
            t_o.append(keep.tile([P, PACK, H], F32, name="t_o%d" % k))
            t_u.append(keep.tile([P, PACK, H], F32, name="t_u%d" % k))
            t_c.append(keep.tile([P, PACK, H], F32, name="t_c%d" % k))
            grad.append(keep.tile([P, PACK, 2 * H], BF16, name="grad%d" % k))

        def load_gate_inputs(lo):
            cols = slice(lo, lo + UNIT)
            for k in range(PASSES):
                nc.sync.dma_start(out=t_o[k][:, :, cols], in_=iou_v[k][:, :, H + lo : H + lo + UNIT])
                nc.sync.dma_start(out=grad[k][:, :, cols], in_=grad_v[k][:, :, cols])
            for k in range(PASSES):
                nc.sync.dma_start(out=t_c[k][:, :, cols], in_=cell_v[k][:, :, cols])
            for k in range(PASSES):
                nc.sync.dma_start(out=grad[k][:, :, H + lo : H + lo + UNIT], in_=grad_v[k][:, :, H + lo : H + lo + UNIT])
            for k in range(PASSES):
                nc.sync.dma_start(out=t_i[k][:, :, cols], in_=iou_v[k][:, :, cols])
            for k in range(PASSES):
                nc.sync.dma_start(out=t_u[k][:, :, cols], in_=iou_v[k][:, :, 2 * H + lo : 2 * H + lo + UNIT])

        both = range(PASSES)
        ctx.enter_context(tc.manual_schedule(engines={mybir.EngineType.DVE, mybir.EngineType.SP}))

        sum_t = {}
        two_max_t = {}
        turned = {}
        grouped = {}

        def mailbox_load(k, g):
            if g == 0:
                sum_t[k] = [
                    psum.tile([P, PASS_NODES], F32, name="sum_t%d" % q, tag="bank", bufs=BANKS) for q in range(H_BLOCKS)
                ]
                two_max_t[k] = pipe.tile([P, W_BLOCKS, E_HALF, P], F32, name="two_max_t")
            pairs = stream.tile([P, PAIR_TILES, SIDE, H], BF16)
            nc.sync.dma_start(out=pairs[:], in_=pair_v[k * LOADS + g])
            pair_max = pipe.tile([P, PAIR_TILES, H], BF16)
            nc.vector.tensor_tensor(out=pair_max[:], in0=pairs[:, :, 0, :], in1=pairs[:, :, 1, :], op=MAX)
            for q in range(H_BLOCKS):
                for t in range(PAIR_TILES):
                    first = (g * PAIR_TILES + t) * PAIR_NODES
                    for b in range(SIDE):
                        nc.tensor.matmul(
                            out=sum_t[k][q][:, first : first + PAIR_NODES],
                            lhsT=pairs[:, t, b, q * P : (q + 1) * P],
                            rhs=pick[:],
                            start=(b == 0),
                            stop=(b == SIDE - 1),
                        )
            pair_max_words = pair_max[:].bitcast(F32)
            p_cols = slice(g * PAIR_TILES * OCTET, (g + 1) * PAIR_TILES * OCTET)
            for q in range(W_BLOCKS):
                turned[(k, g, q)] = psum.tile([P, PAIR_TILES, P], F32, name="turned", tag="bank", bufs=BANKS)
                for t in range(PAIR_TILES):
                    nc.tensor.transpose(
                        out=turned[(k, g, q)][:, t, :], in_=pair_max_words[:, t, q * P : (q + 1) * P], identity=sort[:]
                    )
                nc.scalar.copy(
                    out=two_max_t[k][:, q, :, p_cols].rearrange("h e (t r) -> h e t r", r=OCTET),
                    in_=turned[(k, g, q)][:, :, P // 2 :].rearrange("h t (e r) -> h e t r", r=OCTET),
                )

        def two_max(k, g):
            p_cols = slice(g * PAIR_TILES * OCTET, (g + 1) * PAIR_TILES * OCTET)
            for q in range(W_BLOCKS):
                upper = two_max_t[k][:, q, :, p_cols].bitcast(BF16).rearrange("h e (t x) -> h e t x", x=WORD * OCTET)
                nc.vector.tensor_tensor(
                    out=upper,
                    in0=turned[(k, g, q)][:, :, 0 : P // 2].bitcast(BF16).rearrange("h t (e x) -> h e t x", x=WORD * OCTET),
                    in1=upper,
                    op=MAX,
                )

        def sums_back(k):
            sum_by_hidden = pipe.tile([P, H_BLOCKS, PACK // WORD, WORD * P], BF16, tag="by_hidden")
            for q in range(H_BLOCKS):
                nc.scalar.copy(
                    out=sum_by_hidden[:, q].rearrange("h u (p e) -> h u p e", e=WORD),
                    in_=sum_t[k][q][:].rearrange("h (p u e) -> h u p e", u=PACK // WORD, e=WORD),
                )
            node_words = sum_by_hidden[:].bitcast(F32)
            grouped[(k, 0)] = pipe.tile([P, H, PACK], BF16, name="grouped", align_bytes=64)
            grouped_words = grouped[(k, 0)][:].rearrange("p w j -> p (w j)").bitcast(F32)
            per_bank = H_BLOCKS // W_BLOCKS
            halves = PACK // WORD
            for piece in range(W_BLOCKS):
                back = psum.tile([P, halves, per_bank * P], F32, name="back", tag="bank", bufs=BANKS)
                for u in range(halves):
                    for r in range(per_bank):
                        nc.tensor.transpose(
                            out=back[:, u, r * P : (r + 1) * P],
                            in_=node_words[:, piece * per_bank + r, u, :],
                            identity=ident_f32[:],
                        )
                width = halves * per_bank * P
                nc.scalar.copy(
                    out=grouped_words[:, piece * width : (piece + 1) * width].rearrange("p (w u) -> p w u", u=halves),
                    in_=back[:].rearrange("p u w -> p w u"),
                )

        def max_back(k):
            two = two_max_t[k][:].bitcast(BF16)
            max_by_hidden = pipe.tile([P, W_BLOCKS, PACK, WORD * P], BF16, tag="by_hidden")
            nc.vector.tensor_tensor(out=max_by_hidden[:], in0=two[:, :, 0:PACK, :], in1=two[:, :, PACK:, :], op=MAX)
            words = max_by_hidden[:].bitcast(F32)
            grouped[(k, 1)] = pipe.tile([P, H, PACK], BF16, name="grouped", align_bytes=64)
            for piece in range(W_BLOCKS):
                back = psum.tile([P, PACK, P], F32, name="back", tag="bank", bufs=BANKS)
                for j in range(PACK):
                    nc.tensor.transpose(out=back[:, j, :], in_=words[:, piece, j, :], identity=ident_f32[:])
                w_cols = slice(piece * WORD * P, (piece + 1) * WORD * P)
                nc.scalar.copy(out=grouped[(k, 1)][:, w_cols, :], in_=back[:].bitcast(BF16).rearrange("p j w -> p w j"))

        def quantise_hc(k, half):
            cols = slice(half * H, (half + 1) * H)
            nc.vector.quantize_mx(
                out=hc_codes[:, k, cols].bitcast(E4M3X4),
                scales=hc_scales[:, k, cols],
                in_=grouped[(k, half)][:].rearrange("p w j -> p (w j)"),
            )

        def multiply_and_store(gate, lo):
            vector_helps = gate == 0 and lo + UNIT == H
            for m in range(lo, lo + UNIT, P):
                for n in range(2 * H // BANK):
                    n_cols = slice(n * BANK, (n + 1) * BANK)
                    acc = psum.tile([P, BANK], F32, tag="bank", bufs=BANKS)
                    for k in both:
                        nc.tensor.matmul_mx(
                            out=acc[:],
                            lhsT=d_codes[:, k, gate, m : m + P].bitcast(E5M2X4),
                            lhsT_scale=d_scales[:, k, gate, m : m + P],
                            rhs=hc_codes[:, k, n_cols].bitcast(E4M3X4),
                            rhs_scale=hc_scales[:, k, n_cols],
                            start=(k == 0),
                            stop=(k == PASSES - 1),
                        )
                    result = pipe.tile([P, BANK], F32, bufs=RESULT_BUFS)
                    if vector_helps and n % 2 == 1:
                        nc.vector.tensor_copy(out=result[:], in_=acc[:])
                    else:
                        nc.scalar.copy(out=result[:], in_=acc[:])
                    nc.sync.dma_start(out=out[gate * H + m : gate * H + m + P, n_cols], in_=result[:])

        block = [P, PACK, UNIT]
        grouped_block = [P, UNIT, PACK]

        def chain(lo, by_scalar):
            cols = slice(lo, lo + UNIT)
            tanh_i = [t_i[k][:, :, cols] for k in both]
            tanh_o = [t_o[k][:, :, cols] for k in both]
            tanh_u = [t_u[k][:, :, cols] for k in both]
            tanh_c = [t_c[k][:, :, cols] for k in both]
            g_h = [grad[k][:, :, cols] for k in both]
            g_c = [grad[k][:, :, H + lo : H + lo + UNIT] for k in both]
            sq_c = [pipe.tile(block, F32, name="sq_c%d" % k, bufs=1) for k in both]
            sq_u = [pipe.tile(block, F32, name="sq_u%d" % k, bufs=1) for k in both]
            gh_so = [pipe.tile(block, F32, name="gh_so%d" % k, bufs=1) for k in both]
            d = {
                gate: [pipe.tile(grouped_block, BF16, name="d%d%d" % (gate, k), bufs=1, align_bytes=64) for k in both]
                for gate in range(3)
            }
            def product(dst, in0, scalar, in1, op0, op1):
                nc.vector.scalar_tensor_tensor(out=dst, in0=in0, scalar=scalar, in1=in1, op0=op0, op1=op1)

            def grouped_product(gate, k, in0, scalar, in1, op0, op1):
                if gate in by_scalar:
                    flat = pipe.tile(block, BF16, name="flat%d%d" % (gate, k), bufs=1)
                    product(flat[:], in0, scalar, in1, op0, op1)
                    nc.scalar.copy(out=d[gate][k][:], in_=flat[:].rearrange("p j c -> p c j"))
                else:
                    product(d[gate][k][:], in0.rearrange("p j c -> p c j"), scalar, in1.rearrange("p j c -> p c j"), op0, op1)

            def quantise(gate, k):
                nc.vector.quantize_mx(
                    out=d_codes[:, k, gate, cols].bitcast(E5M2X4),
                    scales=d_scales[:, k, gate, cols],
                    in_=d[gate][k][:].rearrange("p c j -> p (c j)"),
                )

            def step(name, k):
                x = sq_c[k][:]
                if name == "tanh_o":
                    nc.scalar.activation(out=tanh_o[k], in_=tanh_o[k], func=TANH, scale=-0.5)
                elif name == "tanh_c":
                    nc.scalar.activation(out=tanh_c[k], in_=tanh_c[k], func=TANH)
                elif name == "sq_c":
                    nc.scalar.activation(out=x, in_=tanh_c[k], func=SQUARE, scale=0.5)
                elif name == "tanh_i":
                    nc.scalar.activation(out=tanh_i[k], in_=tanh_i[k], func=TANH, scale=-0.5)
                elif name == "tanh_u":
                    nc.scalar.activation(out=tanh_u[k], in_=tanh_u[k], func=TANH)
                elif name == "sq_u":
                    nc.scalar.activation(out=sq_u[k][:], in_=tanh_u[k], func=SQUARE)
                elif name == "gh_so":
                    product(gh_so[k][:], tanh_o[k], -1.0, g_h[k], ADD, MULT)
                elif name == "gh_dso":
                    product(tanh_o[k], tanh_o[k], 1.0, gh_so[k][:], ADD, MULT)
                elif name == "d_o":
                    grouped_product(1, k, tanh_o[k], -0.25, tanh_c[k], MULT, MULT)
                elif name == "through_h":
                    product(x, x, -0.25, gh_so[k][:], ADD, MULT)
                elif name == "half_dc":
                    product(x, g_c[k], 0.5, x, MULT, ADD)
                elif name == "dc_si":
                    product(x, tanh_i[k], -1.0, x, ADD, MULT)
                elif name == "d_u":
                    grouped_product(2, k, sq_u[k][:], -1.0, x, ADD, MULT)
                elif name == "dc_dsi":
                    product(tanh_i[k], tanh_i[k], 1.0, x, ADD, MULT)
                elif name == "d_i":
                    grouped_product(0, k, tanh_i[k], -0.5, tanh_u[k], MULT, MULT)
                elif name == "q_o":
                    quantise(1, k)
                elif name == "q_u":
                    quantise(2, k)
                else:
                    quantise(0, k)

            return step

        def steps(step, names):
            for name in names:
                for k in both:
                    step(name, k)

        load_gate_inputs(0)
        first = chain(0, (1, 2))
        steps(first, ("tanh_o", "tanh_c", "sq_c", "tanh_i", "tanh_u", "sq_u"))
        steps(first, ("gh_so", "gh_dso", "d_o", "through_h", "half_dc", "dc_si", "d_u", "q_o"))
        rest = [(name, k) for name in ("dc_dsi", "q_u", "d_i", "q_i") for k in both]
        loads = [(k, g) for k in both for g in range(LOADS)]
        for n in range(len(loads)):
            mailbox_load(loads[n][0], loads[n][1])
            first(rest[n][0], rest[n][1])
            if n > 0:
                two_max(loads[n - 1][0], loads[n - 1][1])
            if n == LOADS:
                max_back(0)
            if n == LOADS - 1:
                sums_back(0)
            if n == LOADS + 1:
                quantise_hc(0, 0)
            if n == LOADS + 2:
                quantise_hc(0, 1)
        load_gate_inputs(UNIT)
        second = chain(UNIT, ())
        sums_back(PASSES - 1)
        steps(second, ("tanh_o", "gh_so"))
        two_max(PASSES - 1, LOADS - 1)
        max_back(PASSES - 1)
        steps(second, ("gh_dso", "tanh_c", "sq_c"))
        quantise_hc(PASSES - 1, 0)
        steps(second, ("d_o",))
        quantise_hc(PASSES - 1, 1)
        steps(second, ("tanh_i", "tanh_u", "sq_u"))
        for gate in (1, 2, 0):
            multiply_and_store(gate, 0)
        steps(second, ("through_h", "q_o"))
        multiply_and_store(1, UNIT)
        steps(second, ("half_dc", "dc_si", "d_u", "dc_dsi", "q_u"))
        multiply_and_store(2, UNIT)
        steps(second, ("d_i", "q_i"))
        multiply_and_store(0, UNIT)
